import numpy as np
import ml_dtypes


def mxq(x, axis, fmt="e4m3"):
    dtype, down = {"e4m3": (ml_dtypes.float8_e4m3fn, 7), "e5m2": (ml_dtypes.float8_e5m2, 14)}[fmt]
    v = np.moveaxis(np.asarray(x, np.float32).astype(ml_dtypes.bfloat16).astype(np.float64), axis, -1)
    blocks = v.reshape(v.shape[:-1] + (-1, 32))
    amax = np.abs(blocks).max(-1, keepdims=True)
    byte = np.maximum(np.where(amax > 0, np.frexp(amax)[1] - 1 + 127, 0) - down, 1)
    scale = np.exp2(byte - 127.0)
    codes = (blocks / scale).astype(np.float32).astype(dtype).astype(np.float64)
    return np.moveaxis((codes * scale).reshape(v.shape), -1, axis)


WIDE = False


def mx_kscale(k):
    if not WIDE:
        return np.ones(k)
    levels = np.array([10, -10, 5, -5, 0])
    a = np.random.permutation(np.resize(levels, k // 512 * 4)).reshape(k // 512, 4)
    idx = np.arange(k)
    return np.exp2(a[idx // 512, idx % 128 // 32])


BF16 = ml_dtypes.bfloat16


def bf(x):
    return np.asarray(x, np.float32).astype(BF16)


def f64(x):
    return np.asarray(x).astype(np.float64)


B, N_I, N_H1, N_H2, N_H3, N_H4 = 4096, 768, 256, 1024, 2048, 1024
K1 = N_I + N_H1


def sigmoid(v):
    return 1.0 / (1.0 + np.exp(-v))


def setup_inputs():
    s = mx_kscale(K1)

    def w(gain):
        return bf(np.random.standard_normal((N_H1, K1)) * gain / np.sqrt(K1) / s[None, :])

    def b():
        return bf(np.random.standard_normal(N_H1) * 0.3)

    return {"X": bf(np.random.standard_normal((B, N_I)) * s[:N_I]),
            "hidden1": bf(np.random.standard_normal((B, N_H1)) * s[N_I:]),
            "cell1": bf(np.random.standard_normal((B, N_H1))),
            "Wf1": w(1.0), "bf1": b(), "Wi1": w(1.0), "bi1": b(),
            "Wc1": w(5.0 / 3.0), "bc1": b(), "Wo1": w(1.0), "bo1": b()}


def reference(X, hidden1, cell1, Wf1, bf1, Wi1, bi1, Wc1, bc1, Wo1, bo1):
    zq = mxq(np.concatenate([f64(X), f64(hidden1)], axis=1), 1, "e4m3")
    f = sigmoid((zq @ mxq(f64(Wf1), 1, "e4m3").T) + f64(bf1))
    i = sigmoid((zq @ mxq(f64(Wi1), 1, "e4m3").T) + f64(bi1))
    cand = np.tanh((zq @ mxq(f64(Wc1), 1, "e4m3").T) + f64(bc1))
    o = sigmoid((zq @ mxq(f64(Wo1), 1, "e4m3").T) + f64(bo1))
    h_new = o * np.tanh(cand)
    c_new = f * f64(cell1) + cand * i
    return h_new, c_new

@@ -1,0 +1,203 @@
+from contextlib import ExitStack
+
+import concourse.mybir as mybir
+from concourse.masks import make_identity
+
+F32 = mybir.dt.float32
+BF16 = mybir.dt.bfloat16
+U32 = mybir.dt.uint32
+U8 = mybir.dt.uint8
+FP8X4 = mybir.dt.float8_e4m3fn_x4
+ACT = mybir.ActivationFunctionType
+ALU = mybir.AluOpType
+
+P = 128
+PACK = 4
+K = 1024
+N_X = 768
+K_PASS = P * PACK
+PASSES = K // K_PASS
+PASS_WORDS = K_PASS // 2
+BATCH = 4096
+CHUNK = 512
+ROW_TILES = CHUNK // P
+N_CHUNKS = BATCH // CHUNK
+HID = 256
+HALVES = HID // P
+GATES = ("cand", "i", "o", "f")
+GATE_FUNC = {"cand": ACT.Tanh, "i": ACT.Sigmoid, "o": ACT.Sigmoid, "f": ACT.Sigmoid}
+
+FLOPS = 2 * BATCH * K * 4 * HID
+
+
+def tile_quest_pa_t_kernel(
+    tc, X, hidden1, cell1, Wf1, bf1, Wi1, bi1, Wc1, bc1, Wo1, bo1, out_0, out_1
+):
+    nc = tc.nc
+    weights = {"f": Wf1, "i": Wi1, "cand": Wc1, "o": Wo1}
+    biases = {"f": bf1, "i": bi1, "cand": bc1, "o": bo1}
+
+    with ExitStack() as pools:
+        const = pools.enter_context(tc.tile_pool(name="const", bufs=1))
+        w_pool = pools.enter_context(tc.tile_pool(name="w_raw", bufs=len(GATES)))
+        in_pool = pools.enter_context(tc.tile_pool(name="inputs", bufs=N_CHUNKS))
+        grouped_pool = pools.enter_context(tc.tile_pool(name="grouped", bufs=3))
+        codes_pool = pools.enter_context(tc.tile_pool(name="codes", bufs=2))
+        gate_pool = pools.enter_context(tc.tile_pool(name="gates", bufs=2))
+        out_pool = pools.enter_context(tc.tile_pool(name="outs", bufs=3))
+        fwd_psum = pools.enter_context(tc.psum_pool(name="fwd", bufs=2))
+        acc_psum = pools.enter_context(tc.psum_pool(name="acc", bufs=3))
+        back_psum = pools.enter_context(tc.psum_pool(name="back", bufs=3))
+
+        ident = const.tile([P, P], F32)
+        make_identity(nc, ident[:])
+        warm_in = const.tile([P, 1], F32)
+        warm_out = const.tile([P, 1], F32)
+        nc.vector.memset(warm_in[:], 0.0)
+        nc.scalar.activation(out=warm_out[:], in_=warm_in[:], func=ACT.Sigmoid)
+
+        bias_rows = const.tile([P, P], BF16)
+        nc.vector.memset(bias_rows[:], 0.0)
+        for gi, gate in enumerate(GATES):
+            nc.scalar.dma_start(
+                out=bias_rows[HALVES * gi : HALVES * (gi + 1), :],
+                in_=biases[gate].rearrange("(e p) -> e p", p=P),
+            )
+
+        z_rows = []
+        cell_rows = []
+
+        def load_chunk(c):
+            rows = slice(c * CHUNK, (c + 1) * CHUNK)
+            z_sb = in_pool.tile([P, ROW_TILES, K], BF16)
+            nc.sync.dma_start(
+                out=z_sb[:, :, 0:N_X], in_=X[rows, :].rearrange("(p t) k -> p t k", t=ROW_TILES)
+            )
+            nc.sync.dma_start(
+                out=z_sb[:, :, N_X:K], in_=hidden1[rows, :].rearrange("(p t) k -> p t k", t=ROW_TILES)
+            )
+            cell_sb = in_pool.tile([P, ROW_TILES, HID], BF16)
+            nc.sync.dma_start(
+                out=cell_sb[:], in_=cell1[rows, :].rearrange("(p t) h -> p t h", t=ROW_TILES)
+            )
+            z_rows.append(z_sb)
+            cell_rows.append(cell_sb)
+
+        load_chunk(0)
+        w_rows = {}
+        for gate in GATES:
+            w_sb = w_pool.tile([P, HALVES, K], BF16)
+            nc.sync.dma_start(out=w_sb[:], in_=weights[gate].rearrange("(e p) k -> p e k", p=P))
+            w_rows[gate] = w_sb
+        for c in range(1, N_CHUNKS):
+            load_chunk(c)
+
+        def quantise_pass(rows_sb, n_row_tiles, g, codes, scales, pairs_on_scalar):
+            n_cols = n_row_tiles * P
+            grouped = grouped_pool.tile([P, n_cols * PACK], BF16, align_bytes=64)
+            grouped_words = grouped[:].bitcast(F32).rearrange("p (j u) -> p j u", u=2)
+            for pair in range(n_row_tiles // 2):
+                turned = fwd_psum.tile([P, 2, 2 * P], F32)
+                for u in range(2):
+                    first = PASS_WORDS * g + P * u
+                    for r in range(2):
+                        words = rows_sb[:, 2 * pair + r, :].bitcast(F32)
+                        nc.tensor.transpose(
+                            turned[:, u, r * P : (r + 1) * P], words[:, first : first + P], ident[:]
+                        )
+                dst = grouped_words[:, 2 * pair * P : 2 * (pair + 1) * P, :]
+                src = turned[:].rearrange("p u j -> p j u")
+                if pair in pairs_on_scalar:
+                    nc.scalar.copy(out=dst, in_=src)
+                else:
+                    nc.vector.tensor_copy(out=dst, in_=src)
+            nc.vector.quantize_mx(out=codes.bitcast(FP8X4), scales=scales, in_=grouped[:])
+
+        def new_z_codes():
+            z_codes = codes_pool.tile([P, PASSES, CHUNK], U32, align_bytes=64)
+            z_scales = codes_pool.tile([P, PASSES, CHUNK], U8, align_bytes=64)
+            return z_codes, z_scales
+
+        def compute_gates(z_codes, z_scales, half):
+            cols = slice(half * P, (half + 1) * P)
+            val = {}
+            for gi, gate in enumerate(GATES):
+                acc = acc_psum.tile([P, CHUNK], F32)
+                for g in range(PASSES):
+                    nc.tensor.matmul_mx(
+                        out=acc[:],
+                        lhsT=w_codes[:, gi, g, cols].bitcast(FP8X4),
+                        lhsT_scale=w_scales[:, gi, g, cols],
+                        rhs=z_codes[:, g, :].bitcast(FP8X4),
+                        rhs_scale=z_scales[:, g, :],
+                        start=(g == 0),
+                        stop=(g == PASSES - 1),
+                    )
+                gate_sb = gate_pool.tile([P, CHUNK], F32, tag="gate_" + gate)
+                col = HALVES * gi + half
+                nc.scalar.activation(
+                    out=gate_sb[:], in_=acc[:], func=GATE_FUNC[gate], bias=bias_sb[:, col : col + 1], scale=1.0
+                )
+                val[gate] = gate_sb
+                if gate == "i":
+                    tanh_cand = gate_pool.tile([P, CHUNK], F32)
+                    nc.scalar.activation(out=tanh_cand[:], in_=val["cand"][:], func=ACT.Tanh)
+                    cand_i = gate_pool.tile([P, CHUNK], F32)
+                    nc.vector.tensor_tensor(out=cand_i[:], in0=val["cand"][:], in1=val["i"][:], op=ALU.mult)
+            h_turned = gate_pool.tile([P, CHUNK], F32)
+            nc.vector.tensor_tensor(out=h_turned[:], in0=val["o"][:], in1=tanh_cand[:], op=ALU.mult)
+            return val["f"], cand_i, h_turned
+
+        def turn_back(src):
+            back = back_psum.tile([P, ROW_TILES, P], F32)
+            for t in range(ROW_TILES):
+                nc.tensor.transpose(back[:, t, :], src[:, t * P : (t + 1) * P], ident[:])
+            return back
+
+        def finish(c, half, f_gate, cand_i, h_turned, h_sb, c_sb):
+            cols = slice(half * P, (half + 1) * P)
+            f_back = turn_back(f_gate)
+            ci_back = turn_back(cand_i)
+            h_back = turn_back(h_turned)
+            f_cell = out_pool.tile([P, ROW_TILES, P], F32)
+            nc.vector.tensor_tensor(out=f_cell[:], in0=f_back[:], in1=cell_rows[c][:, :, cols], op=ALU.mult)
+            nc.scalar.copy(out=h_sb[:, :, cols], in_=h_back[:])
+            nc.vector.tensor_tensor(out=c_sb[:, :, cols], in0=ci_back[:], in1=f_cell[:], op=ALU.add)
+            if half == HALVES - 1:
+                rows = slice(c * CHUNK, (c + 1) * CHUNK)
+                nc.sync.dma_start(out=out_0[rows, :].rearrange("(p t) h -> p t h", t=ROW_TILES), in_=h_sb[:])
+                nc.sync.dma_start(out=out_1[rows, :].rearrange("(p t) h -> p t h", t=ROW_TILES), in_=c_sb[:])
+
+        bias_rows_f32 = const.tile([P, P], F32)
+        nc.vector.tensor_copy(out=bias_rows_f32[:], in_=bias_rows[:])
+        bias_ps = back_psum.tile([P, P], F32, tag="back")
+        nc.tensor.transpose(bias_ps[:], bias_rows_f32[:], ident[:])
+        bias_sb = const.tile([P, HALVES * len(GATES)], F32)
+        nc.vector.tensor_copy(out=bias_sb[:], in_=bias_ps[:, 0 : HALVES * len(GATES)])
+
+        z_codes, z_scales = new_z_codes()
+        for g in range(PASSES):
+            quantise_pass(z_rows[0], ROW_TILES, g, z_codes[:, g, :], z_scales[:, g, :], (1,))
+        w_codes = const.tile([P, len(GATES), PASSES, HID], U32, align_bytes=64)
+        w_scales = const.tile([P, len(GATES), PASSES, HID], U8, align_bytes=64)
+        for gi, gate in enumerate(GATES):
+            for g in range(PASSES):
+                quantise_pass(w_rows[gate], HALVES, g, w_codes[:, gi, g, :], w_scales[:, gi, g, :], (0,) if g == 1 else ())
+
+        waiting = None
+        for c in range(N_CHUNKS):
+            h_sb = out_pool.tile([P, ROW_TILES, HID], F32)
+            c_sb = out_pool.tile([P, ROW_TILES, HID], F32)
+            if c + 1 < N_CHUNKS:
+                next_codes, next_scales = new_z_codes()
+            for half in range(HALVES):
+                f_gate, cand_i, h_turned = compute_gates(z_codes, z_scales, half)
+                if c + 1 < N_CHUNKS:
+                    g = half
+                    quantise_pass(z_rows[c + 1], ROW_TILES, g, next_codes[:, g, :], next_scales[:, g, :], ())
+                if waiting is not None:
+                    finish(*waiting)
+                waiting = (c, half, f_gate, cand_i, h_turned, h_sb, c_sb)
+            if c + 1 < N_CHUNKS:
+                z_codes, z_scales = next_codes, next_scales
+        finish(*waiting)

@@ -24,6 +24,9 @@ ROW_TILES = CHUNK // P
 N_CHUNKS = BATCH // CHUNK
 HID = 256
 HALVES = HID // P
+N_ROUNDS = N_CHUNKS * HALVES
+N_Z_PASSES = N_CHUNKS * PASSES
+AHEAD = 3
 GATES = ("cand", "i", "o", "f")
 GATE_FUNC = {"cand": ACT.Tanh, "i": ACT.Sigmoid, "o": ACT.Sigmoid, "f": ACT.Sigmoid}
 
@@ -37,24 +40,18 @@ def tile_quest_pa_t_kernel(
     weights = {"f": Wf1, "i": Wi1, "cand": Wc1, "o": Wo1}
     biases = {"f": bf1, "i": bi1, "cand": bc1, "o": bo1}
 
-    with ExitStack() as pools:
-        const = pools.enter_context(tc.tile_pool(name="const", bufs=1))
-        w_pool = pools.enter_context(tc.tile_pool(name="w_raw", bufs=len(GATES)))
-        in_pool = pools.enter_context(tc.tile_pool(name="inputs", bufs=N_CHUNKS))
-        grouped_pool = pools.enter_context(tc.tile_pool(name="grouped", bufs=3))
-        codes_pool = pools.enter_context(tc.tile_pool(name="codes", bufs=2))
-        gate_pool = pools.enter_context(tc.tile_pool(name="gates", bufs=2))
-        out_pool = pools.enter_context(tc.tile_pool(name="outs", bufs=3))
-        fwd_psum = pools.enter_context(tc.psum_pool(name="fwd", bufs=2))
-        acc_psum = pools.enter_context(tc.psum_pool(name="acc", bufs=3))
-        back_psum = pools.enter_context(tc.psum_pool(name="back", bufs=3))
-
-        ident = const.tile([P, P], F32)
-        make_identity(nc, ident[:])
-        warm_in = const.tile([P, 1], F32)
-        warm_out = const.tile([P, 1], F32)
-        nc.vector.memset(warm_in[:], 0.0)
-        nc.scalar.activation(out=warm_out[:], in_=warm_in[:], func=ACT.Sigmoid)
+    with ExitStack() as stack:
+        stack.enter_context(tc.manual_schedule())
+        const = stack.enter_context(tc.tile_pool(name="const", bufs=1))
+        w_pool = stack.enter_context(tc.tile_pool(name="w_raw", bufs=len(GATES)))
+        in_pool = stack.enter_context(tc.tile_pool(name="inputs", bufs=N_CHUNKS))
+        grouped_pool = stack.enter_context(tc.tile_pool(name="grouped", bufs=3))
+        codes_pool = stack.enter_context(tc.tile_pool(name="codes", bufs=PASSES + AHEAD))
+        gate_pool = stack.enter_context(tc.tile_pool(name="gates", bufs=2))
+        out_pool = stack.enter_context(tc.tile_pool(name="outs", bufs=3))
+        fwd_psum = stack.enter_context(tc.psum_pool(name="fwd", bufs=2))
+        acc_psum = stack.enter_context(tc.psum_pool(name="acc", bufs=4))
+        back_psum = stack.enter_context(tc.psum_pool(name="back", bufs=2))
 
         bias_rows = const.tile([P, P], BF16)
         nc.vector.memset(bias_rows[:], 0.0)
@@ -67,7 +64,7 @@ def tile_quest_pa_t_kernel(
         z_rows = []
         cell_rows = []
 
-        def load_chunk(c):
+        def load_z(c):
             rows = slice(c * CHUNK, (c + 1) * CHUNK)
             z_sb = in_pool.tile([P, ROW_TILES, K], BF16)
             nc.sync.dma_start(
@@ -76,25 +73,36 @@ def tile_quest_pa_t_kernel(
             nc.sync.dma_start(
                 out=z_sb[:, :, N_X:K], in_=hidden1[rows, :].rearrange("(p t) k -> p t k", t=ROW_TILES)
             )
+            z_rows.append(z_sb)
+
+        def load_cell(c):
+            rows = slice(c * CHUNK, (c + 1) * CHUNK)
             cell_sb = in_pool.tile([P, ROW_TILES, HID], BF16)
             nc.sync.dma_start(
                 out=cell_sb[:], in_=cell1[rows, :].rearrange("(p t) h -> p t h", t=ROW_TILES)
             )
-            z_rows.append(z_sb)
             cell_rows.append(cell_sb)
 
-        load_chunk(0)
+        load_z(0)
         w_rows = {}
         for gate in GATES:
             w_sb = w_pool.tile([P, HALVES, K], BF16)
             nc.sync.dma_start(out=w_sb[:], in_=weights[gate].rearrange("(e p) k -> p e k", p=P))
             w_rows[gate] = w_sb
         for c in range(1, N_CHUNKS):
-            load_chunk(c)
+            load_z(c)
+            load_cell(c - 1)
+        load_cell(N_CHUNKS - 1)
 
-        def quantise_pass(rows_sb, n_row_tiles, g, codes, scales, pairs_on_scalar):
-            n_cols = n_row_tiles * P
-            grouped = grouped_pool.tile([P, n_cols * PACK], BF16, align_bytes=64)
+        ident = const.tile([P, P], F32)
+        make_identity(nc, ident[:])
+        warm_in = const.tile([P, 1], F32)
+        warm_out = const.tile([P, 1], F32)
+        nc.vector.memset(warm_in[:], 0.0)
+        nc.scalar.activation(out=warm_out[:], in_=warm_in[:], func=ACT.Sigmoid)
+
+        def turn_pass(rows_sb, n_row_tiles, g, pairs_on_scalar):
+            grouped = grouped_pool.tile([P, n_row_tiles * P * PACK], BF16, align_bytes=64)
             grouped_words = grouped[:].bitcast(F32).rearrange("p (j u) -> p j u", u=2)
             for pair in range(n_row_tiles // 2):
                 turned = fwd_psum.tile([P, 2, 2 * P], F32)
@@ -111,14 +119,26 @@ def tile_quest_pa_t_kernel(
                     nc.scalar.copy(out=dst, in_=src)
                 else:
                     nc.vector.tensor_copy(out=dst, in_=src)
+            return grouped
+
+        def quantise(grouped, codes, scales):
             nc.vector.quantize_mx(out=codes.bitcast(FP8X4), scales=scales, in_=grouped[:])
 
-        def new_z_codes():
-            z_codes = codes_pool.tile([P, PASSES, CHUNK], U32, align_bytes=64)
-            z_scales = codes_pool.tile([P, PASSES, CHUNK], U8, align_bytes=64)
-            return z_codes, z_scales
+        z_codes = []
+        z_scales = []
 
-        def compute_gates(z_codes, z_scales, half):
+        def turn_z_pass(number, pairs_on_scalar):
+            c, g = divmod(number, PASSES)
+            return turn_pass(z_rows[c], ROW_TILES, g, pairs_on_scalar)
+
+        def quantise_z_pass(grouped):
+            codes = codes_pool.tile([P, CHUNK], U32, align_bytes=64)
+            scales = codes_pool.tile([P, CHUNK], U8, align_bytes=64)
+            quantise(grouped, codes[:], scales[:])
+            z_codes.append(codes)
+            z_scales.append(scales)
+
+        def compute_gates(c, half):
             cols = slice(half * P, (half + 1) * P)
             val = {}
             for gi, gate in enumerate(GATES):
@@ -128,8 +148,8 @@ def tile_quest_pa_t_kernel(
                         out=acc[:],
                         lhsT=w_codes[:, gi, g, cols].bitcast(FP8X4),
                         lhsT_scale=w_scales[:, gi, g, cols],
-                        rhs=z_codes[:, g, :].bitcast(FP8X4),
-                        rhs_scale=z_scales[:, g, :],
+                        rhs=z_codes[PASSES * c + g][:].bitcast(FP8X4),
+                        rhs_scale=z_scales[PASSES * c + g][:],
                         start=(g == 0),
                         stop=(g == PASSES - 1),
                     )
@@ -143,9 +163,10 @@ def tile_quest_pa_t_kernel(
                     tanh_cand = gate_pool.tile([P, CHUNK], F32)
                     nc.scalar.activation(out=tanh_cand[:], in_=val["cand"][:], func=ACT.Tanh)
                     cand_i = gate_pool.tile([P, CHUNK], F32)
-                    nc.vector.tensor_tensor(out=cand_i[:], in0=val["cand"][:], in1=val["i"][:], op=ALU.mult)
-            h_turned = gate_pool.tile([P, CHUNK], F32)
-            nc.vector.tensor_tensor(out=h_turned[:], in0=val["o"][:], in1=tanh_cand[:], op=ALU.mult)
+                    nc.gpsimd.tensor_tensor(out=cand_i[:], in0=val["cand"][:], in1=val["i"][:], op=ALU.mult)
+                if gate == "o":
+                    h_turned = gate_pool.tile([P, CHUNK], F32)
+                    nc.gpsimd.tensor_tensor(out=h_turned[:], in0=val["o"][:], in1=tanh_cand[:], op=ALU.mult)
             return val["f"], cand_i, h_turned
 
         def turn_back(src):
@@ -154,19 +175,27 @@ def tile_quest_pa_t_kernel(
                 nc.tensor.transpose(back[:, t, :], src[:, t * P : (t + 1) * P], ident[:])
             return back
 
-        def finish(c, half, f_gate, cand_i, h_turned, h_sb, c_sb):
+        def finish_h_and_f(c, half, f_gate, h_turned, h_sb):
             cols = slice(half * P, (half + 1) * P)
-            f_back = turn_back(f_gate)
-            ci_back = turn_back(cand_i)
             h_back = turn_back(h_turned)
+            f_back = turn_back(f_gate)
+            nc.vector.tensor_copy(out=h_sb[:, :, cols], in_=h_back[:])
             f_cell = out_pool.tile([P, ROW_TILES, P], F32)
             nc.vector.tensor_tensor(out=f_cell[:], in0=f_back[:], in1=cell_rows[c][:, :, cols], op=ALU.mult)
-            nc.scalar.copy(out=h_sb[:, :, cols], in_=h_back[:])
+            return f_cell
+
+        def finish_c(c, half, cand_i, f_cell, c_sb):
+            cols = slice(half * P, (half + 1) * P)
+            ci_back = turn_back(cand_i)
             nc.vector.tensor_tensor(out=c_sb[:, :, cols], in0=ci_back[:], in1=f_cell[:], op=ALU.add)
-            if half == HALVES - 1:
-                rows = slice(c * CHUNK, (c + 1) * CHUNK)
-                nc.sync.dma_start(out=out_0[rows, :].rearrange("(p t) h -> p t h", t=ROW_TILES), in_=h_sb[:])
-                nc.sync.dma_start(out=out_1[rows, :].rearrange("(p t) h -> p t h", t=ROW_TILES), in_=c_sb[:])
+
+        def store(c, h_sb, c_sb):
+            rows = slice(c * CHUNK, (c + 1) * CHUNK)
+            nc.sync.dma_start(out=out_0[rows, :].rearrange("(p t) h -> p t h", t=ROW_TILES), in_=h_sb[:])
+            nc.sync.dma_start(out=out_1[rows, :].rearrange("(p t) h -> p t h", t=ROW_TILES), in_=c_sb[:])
+
+        for number in range(PASSES):
+            quantise_z_pass(turn_z_pass(number, (1,)))
 
         bias_rows_f32 = const.tile([P, P], F32)
         nc.vector.tensor_copy(out=bias_rows_f32[:], in_=bias_rows[:])
@@ -175,29 +204,34 @@ def tile_quest_pa_t_kernel(
         bias_sb = const.tile([P, HALVES * len(GATES)], F32)
         nc.vector.tensor_copy(out=bias_sb[:], in_=bias_ps[:, 0 : HALVES * len(GATES)])
 
-        z_codes, z_scales = new_z_codes()
-        for g in range(PASSES):
-            quantise_pass(z_rows[0], ROW_TILES, g, z_codes[:, g, :], z_scales[:, g, :], (1,))
         w_codes = const.tile([P, len(GATES), PASSES, HID], U32, align_bytes=64)
         w_scales = const.tile([P, len(GATES), PASSES, HID], U8, align_bytes=64)
         for gi, gate in enumerate(GATES):
+            w_grouped = [turn_pass(w_rows[gate], HALVES, g, (0,) if g == 1 else ()) for g in range(PASSES)]
             for g in range(PASSES):
-                quantise_pass(w_rows[gate], HALVES, g, w_codes[:, gi, g, :], w_scales[:, gi, g, :], (0,) if g == 1 else ())
+                quantise(w_grouped[g], w_codes[:, gi, g, :], w_scales[:, gi, g, :])
 
-        waiting = None
-        for c in range(N_CHUNKS):
-            h_sb = out_pool.tile([P, ROW_TILES, HID], F32)
-            c_sb = out_pool.tile([P, ROW_TILES, HID], F32)
-            if c + 1 < N_CHUNKS:
-                next_codes, next_scales = new_z_codes()
-            for half in range(HALVES):
-                f_gate, cand_i, h_turned = compute_gates(z_codes, z_scales, half)
-                if c + 1 < N_CHUNKS:
-                    g = half
-                    quantise_pass(z_rows[c + 1], ROW_TILES, g, next_codes[:, g, :], next_scales[:, g, :], ())
-                if waiting is not None:
-                    finish(*waiting)
-                waiting = (c, half, f_gate, cand_i, h_turned, h_sb, c_sb)
-            if c + 1 < N_CHUNKS:
-                z_codes, z_scales = next_codes, next_scales
-        finish(*waiting)
+        before = None
+        for s in range(N_ROUNDS + 1):
+            if s < N_ROUNDS:
+                c, half = divmod(s, HALVES)
+                if half == 0:
+                    h_sb = out_pool.tile([P, ROW_TILES, HID], F32)
+                    c_sb = out_pool.tile([P, ROW_TILES, HID], F32)
+                f_gate, cand_i, h_turned = compute_gates(c, half)
+            if before is not None:
+                f_cell = finish_h_and_f(before["c"], before["half"], before["f_gate"], before["h_turned"], before["h_sb"])
+            fresh = [
+                turn_z_pass(number, ())
+                for number in range(len(z_codes), min(s + AHEAD, N_Z_PASSES - 1) + 1)
+            ]
+            if before is not None:
+                finish_c(before["c"], before["half"], before["cand_i"], f_cell, before["c_sb"])
+            for grouped in fresh:
+                quantise_z_pass(grouped)
+            if before is not None and before["half"] == HALVES - 1:
+                store(before["c"], before["h_sb"], before["c_sb"])
+            before = {
+                "c": c, "half": half, "f_gate": f_gate, "cand_i": cand_i, "h_turned": h_turned,
+                "h_sb": h_sb, "c_sb": c_sb,
+            }

@@ -12,6 +12,7 @@ ACT = mybir.ActivationFunctionType
 ALU = mybir.AluOpType
 
 P = 128
+PSUM_BANKS = 8
 PACK = 4
 K = 1024
 N_X = 768
@@ -49,9 +50,7 @@ def tile_quest_pa_t_kernel(
         codes_pool = stack.enter_context(tc.tile_pool(name="codes", bufs=PASSES + AHEAD))
         gate_pool = stack.enter_context(tc.tile_pool(name="gates", bufs=2))
         out_pool = stack.enter_context(tc.tile_pool(name="outs", bufs=3))
-        fwd_psum = stack.enter_context(tc.psum_pool(name="fwd", bufs=2))
-        acc_psum = stack.enter_context(tc.psum_pool(name="acc", bufs=4))
-        back_psum = stack.enter_context(tc.psum_pool(name="back", bufs=2))
+        psum = stack.enter_context(tc.psum_pool(name="psum", bufs=PSUM_BANKS))
 
         bias_rows = const.tile([P, P], BF16)
         nc.vector.memset(bias_rows[:], 0.0)
@@ -105,7 +104,7 @@ def tile_quest_pa_t_kernel(
             grouped = grouped_pool.tile([P, n_row_tiles * P * PACK], BF16, align_bytes=64)
             grouped_words = grouped[:].bitcast(F32).rearrange("p (j u) -> p j u", u=2)
             for pair in range(n_row_tiles // 2):
-                turned = fwd_psum.tile([P, 2, 2 * P], F32)
+                turned = psum.tile([P, 2, 2 * P], F32, tag="bank")
                 for u in range(2):
                     first = PASS_WORDS * g + P * u
                     for r in range(2):
@@ -142,7 +141,7 @@ def tile_quest_pa_t_kernel(
             cols = slice(half * P, (half + 1) * P)
             val = {}
             for gi, gate in enumerate(GATES):
-                acc = acc_psum.tile([P, CHUNK], F32)
+                acc = psum.tile([P, CHUNK], F32, tag="bank")
                 for g in range(PASSES):
                     nc.tensor.matmul_mx(
                         out=acc[:],
@@ -170,7 +169,7 @@ def tile_quest_pa_t_kernel(
             return val["f"], cand_i, h_turned
 
         def turn_back(src):
-            back = back_psum.tile([P, ROW_TILES, P], F32)
+            back = psum.tile([P, ROW_TILES, P], F32, tag="bank")
             for t in range(ROW_TILES):
                 nc.tensor.transpose(back[:, t, :], src[:, t * P : (t + 1) * P], ident[:])
             return back
@@ -179,7 +178,7 @@ def tile_quest_pa_t_kernel(
             cols = slice(half * P, (half + 1) * P)
             h_back = turn_back(h_turned)
             f_back = turn_back(f_gate)
-            nc.vector.tensor_copy(out=h_sb[:, :, cols], in_=h_back[:])
+            nc.scalar.copy(out=h_sb[:, :, cols], in_=h_back[:])
             f_cell = out_pool.tile([P, ROW_TILES, P], F32)
             nc.vector.tensor_tensor(out=f_cell[:], in0=f_back[:], in1=cell_rows[c][:, :, cols], op=ALU.mult)
             return f_cell
@@ -199,7 +198,7 @@ def tile_quest_pa_t_kernel(
 
         bias_rows_f32 = const.tile([P, P], F32)
         nc.vector.tensor_copy(out=bias_rows_f32[:], in_=bias_rows[:])
-        bias_ps = back_psum.tile([P, P], F32, tag="back")
+        bias_ps = psum.tile([P, P], F32, tag="bank")
         nc.tensor.transpose(bias_ps[:], bias_rows_f32[:], ident[:])
         bias_sb = const.tile([P, HALVES * len(GATES)], F32)
         nc.vector.tensor_copy(out=bias_sb[:], in_=bias_ps[:, 0 : HALVES * len(GATES)])

@@ -18,7 +18,6 @@ K = 1024
 N_X = 768
 K_PASS = P * PACK
 PASSES = K // K_PASS
-PASS_WORDS = K_PASS // 2
 BATCH = 4096
 CHUNK = 512
 ROW_TILES = CHUNK // P
@@ -26,10 +25,11 @@ N_CHUNKS = BATCH // CHUNK
 HID = 256
 HALVES = HID // P
 N_ROUNDS = N_CHUNKS * HALVES
-N_Z_PASSES = N_CHUNKS * PASSES
+N_PAIRS = N_CHUNKS * 2
 AHEAD = 3
 GATES = ("cand", "i", "o", "f")
-GATE_FUNC = {"cand": ACT.Tanh, "i": ACT.Sigmoid, "o": ACT.Sigmoid, "f": ACT.Sigmoid}
+TURNED_GATES = ("cand", "i", "o")
+GATE_FUNC = {"cand": ACT.Tanh, "i": ACT.Sigmoid, "o": ACT.Sigmoid}
 
 FLOPS = 2 * BATCH * K * 4 * HID
 
@@ -44,10 +44,10 @@ def tile_quest_pa_t_kernel(
     with ExitStack() as stack:
         stack.enter_context(tc.manual_schedule())
         const = stack.enter_context(tc.tile_pool(name="const", bufs=1))
-        w_pool = stack.enter_context(tc.tile_pool(name="w_raw", bufs=len(GATES)))
+        w_pool = stack.enter_context(tc.tile_pool(name="w_raw", bufs=len(GATES) * HALVES))
         in_pool = stack.enter_context(tc.tile_pool(name="inputs", bufs=N_CHUNKS))
-        grouped_pool = stack.enter_context(tc.tile_pool(name="grouped", bufs=3))
-        codes_pool = stack.enter_context(tc.tile_pool(name="codes", bufs=PASSES + AHEAD))
+        grouped_pool = stack.enter_context(tc.tile_pool(name="grouped", bufs=2))
+        codes_pool = stack.enter_context(tc.tile_pool(name="codes", bufs=3))
         gate_pool = stack.enter_context(tc.tile_pool(name="gates", bufs=2))
         out_pool = stack.enter_context(tc.tile_pool(name="outs", bufs=3))
         psum = stack.enter_context(tc.psum_pool(name="psum", bufs=PSUM_BANKS))
@@ -62,6 +62,7 @@ def tile_quest_pa_t_kernel(
 
         z_rows = []
         cell_rows = []
+        w_rows = {}
 
         def load_z(c):
             rows = slice(c * CHUNK, (c + 1) * CHUNK)
@@ -82,12 +83,16 @@ def tile_quest_pa_t_kernel(
             )
             cell_rows.append(cell_sb)
 
+        def load_w(gate, half):
+            w_sb = w_pool.tile([P, K], BF16)
+            nc.sync.dma_start(out=w_sb[:], in_=weights[gate][half * P : (half + 1) * P, :])
+            w_rows[(gate, half)] = w_sb
+
+        w_for_round_0 = [(gate, 0) for gate in TURNED_GATES] + [("f", 0), ("f", 1)]
+        w_for_round_1 = [(gate, 1) for gate in TURNED_GATES]
         load_z(0)
-        w_rows = {}
-        for gate in GATES:
-            w_sb = w_pool.tile([P, HALVES, K], BF16)
-            nc.sync.dma_start(out=w_sb[:], in_=weights[gate].rearrange("(e p) k -> p e k", p=P))
-            w_rows[gate] = w_sb
+        for gate, half in w_for_round_0 + w_for_round_1:
+            load_w(gate, half)
         for c in range(1, N_CHUNKS):
             load_z(c)
             load_cell(c - 1)
@@ -100,55 +105,72 @@ def tile_quest_pa_t_kernel(
         nc.vector.memset(warm_in[:], 0.0)
         nc.scalar.activation(out=warm_out[:], in_=warm_in[:], func=ACT.Sigmoid)
 
-        def turn_pass(rows_sb, n_row_tiles, g, pairs_on_scalar):
-            grouped = grouped_pool.tile([P, n_row_tiles * P * PACK], BF16, align_bytes=64)
-            grouped_words = grouped[:].bitcast(F32).rearrange("p (j u) -> p j u", u=2)
-            for pair in range(n_row_tiles // 2):
-                turned = psum.tile([P, 2, 2 * P], F32, tag="bank")
+        def words_view(grouped):
+            return grouped[:].bitcast(F32).rearrange("p (g j u) -> p g j u", g=PASSES, u=2)
+
+        def turn_rows(rows, dst_words, on_scalar):
+            bank = psum.tile([P, PASSES, 2, P], F32, tag="bank")
+            words = rows.bitcast(F32)
+            for g in range(PASSES):
                 for u in range(2):
-                    first = PASS_WORDS * g + P * u
-                    for r in range(2):
-                        words = rows_sb[:, 2 * pair + r, :].bitcast(F32)
-                        nc.tensor.transpose(
-                            turned[:, u, r * P : (r + 1) * P], words[:, first : first + P], ident[:]
-                        )
-                dst = grouped_words[:, 2 * pair * P : 2 * (pair + 1) * P, :]
-                src = turned[:].rearrange("p u j -> p j u")
-                if pair in pairs_on_scalar:
-                    nc.scalar.copy(out=dst, in_=src)
-                else:
-                    nc.vector.tensor_copy(out=dst, in_=src)
-            return grouped
+                    first = (2 * g + u) * P
+                    nc.tensor.transpose(bank[:, g, u, :], words[:, first : first + P], ident[:])
+            src = bank[:].rearrange("p g u j -> p g j u")
+            if on_scalar:
+                nc.scalar.copy(out=dst_words, in_=src)
+            else:
+                nc.vector.tensor_copy(out=dst_words, in_=src)
 
-        def quantise(grouped, codes, scales):
-            nc.vector.quantize_mx(out=codes.bitcast(FP8X4), scales=scales, in_=grouped[:])
+        def quantise(grouped, n_cols, g, codes, scales):
+            values = grouped[:, g * n_cols * PACK : (g + 1) * n_cols * PACK]
+            nc.vector.quantize_mx(out=codes.bitcast(FP8X4), scales=scales, in_=values)
 
+        w_codes = const.tile([P, len(GATES), PASSES, HID], U32, align_bytes=64)
+        w_scales = const.tile([P, len(GATES), PASSES, HID], U8, align_bytes=64)
+
+        def prepare_w(gate, half, on_scalar):
+            w_grouped = grouped_pool.tile([P, PASSES * P * PACK], BF16, align_bytes=64)
+            turn_rows(w_rows[(gate, half)][:], words_view(w_grouped), on_scalar)
+            gi = GATES.index(gate)
+            cols = slice(half * P, (half + 1) * P)
+            for g in range(PASSES):
+                quantise(w_grouped, P, g, w_codes[:, gi, g, cols], w_scales[:, gi, g, cols])
+
+        z_grouped = []
         z_codes = []
         z_scales = []
 
-        def turn_z_pass(number, pairs_on_scalar):
-            c, g = divmod(number, PASSES)
-            return turn_pass(z_rows[c], ROW_TILES, g, pairs_on_scalar)
+        def turn_z_pair(m, second_on_scalar):
+            c, part = divmod(m, 2)
+            if part == 0:
+                grouped = grouped_pool.tile([P, PASSES * CHUNK * PACK], BF16, align_bytes=64)
+                z_grouped.append(grouped)
+            for r in range(2):
+                t = 2 * part + r
+                dst_words = words_view(z_grouped[c])[:, :, t * P : (t + 1) * P, :]
+                turn_rows(z_rows[c][:, t, :], dst_words, second_on_scalar and r == 1)
 
-        def quantise_z_pass(grouped):
-            codes = codes_pool.tile([P, CHUNK], U32, align_bytes=64)
-            scales = codes_pool.tile([P, CHUNK], U8, align_bytes=64)
-            quantise(grouped, codes[:], scales[:])
+        def quantise_z(c):
+            codes = codes_pool.tile([P, PASSES, CHUNK], U32, align_bytes=64)
+            scales = codes_pool.tile([P, PASSES, CHUNK], U8, align_bytes=64)
+            for g in range(PASSES):
+                quantise(z_grouped[c], CHUNK, g, codes[:, g, :], scales[:, g, :])
             z_codes.append(codes)
             z_scales.append(scales)
 
-        def compute_gates(c, half):
+        def turned_gates(c, half):
             cols = slice(half * P, (half + 1) * P)
             val = {}
-            for gi, gate in enumerate(GATES):
+            for gate in TURNED_GATES:
+                gi = GATES.index(gate)
                 acc = psum.tile([P, CHUNK], F32, tag="bank")
                 for g in range(PASSES):
                     nc.tensor.matmul_mx(
                         out=acc[:],
                         lhsT=w_codes[:, gi, g, cols].bitcast(FP8X4),
                         lhsT_scale=w_scales[:, gi, g, cols],
-                        rhs=z_codes[PASSES * c + g][:].bitcast(FP8X4),
-                        rhs_scale=z_scales[PASSES * c + g][:],
+                        rhs=z_codes[c][:, g, :].bitcast(FP8X4),
+                        rhs_scale=z_scales[c][:, g, :],
                         start=(g == 0),
                         stop=(g == PASSES - 1),
                     )
@@ -163,10 +185,34 @@ def tile_quest_pa_t_kernel(
                     nc.scalar.activation(out=tanh_cand[:], in_=val["cand"][:], func=ACT.Tanh)
                     cand_i = gate_pool.tile([P, CHUNK], F32)
                     nc.gpsimd.tensor_tensor(out=cand_i[:], in0=val["cand"][:], in1=val["i"][:], op=ALU.mult)
-                if gate == "o":
-                    h_turned = gate_pool.tile([P, CHUNK], F32)
-                    nc.gpsimd.tensor_tensor(out=h_turned[:], in0=val["o"][:], in1=tanh_cand[:], op=ALU.mult)
-            return val["f"], cand_i, h_turned
+            h_turned = gate_pool.tile([P, CHUNK], F32)
+            nc.gpsimd.tensor_tensor(out=h_turned[:], in0=val["o"][:], in1=tanh_cand[:], op=ALU.mult)
+            return cand_i, h_turned
+
+        def forget_sums(c):
+            gi = GATES.index("f")
+            f_gate = gate_pool.tile([P, ROW_TILES, HID], F32)
+            for part in range(2):
+                acc = psum.tile([P, 2, HID], F32, tag="bank")
+                for r in range(2):
+                    cols = slice((2 * part + r) * P, (2 * part + r + 1) * P)
+                    for g in range(PASSES):
+                        nc.tensor.matmul_mx(
+                            out=acc[:, r, :],
+                            lhsT=z_codes[c][:, g, cols].bitcast(FP8X4),
+                            lhsT_scale=z_scales[c][:, g, cols],
+                            rhs=w_codes[:, gi, g, :].bitcast(FP8X4),
+                            rhs_scale=w_scales[:, gi, g, :],
+                            start=(g == 0),
+                            stop=(g == PASSES - 1),
+                        )
+                nc.vector.tensor_tensor(
+                    out=f_gate[:, 2 * part : 2 * part + 2, :],
+                    in0=acc[:],
+                    in1=bias_f[:].unsqueeze(1).to_broadcast([P, 2, HID]),
+                    op=ALU.add,
+                )
+            return f_gate
 
         def turn_back(src):
             back = psum.tile([P, ROW_TILES, P], F32, tag="bank")
@@ -174,27 +220,10 @@ def tile_quest_pa_t_kernel(
                 nc.tensor.transpose(back[:, t, :], src[:, t * P : (t + 1) * P], ident[:])
             return back
 
-        def finish_h_and_f(c, half, f_gate, h_turned, h_sb):
-            cols = slice(half * P, (half + 1) * P)
-            h_back = turn_back(h_turned)
-            f_back = turn_back(f_gate)
-            nc.scalar.copy(out=h_sb[:, :, cols], in_=h_back[:])
-            f_cell = out_pool.tile([P, ROW_TILES, P], F32)
-            nc.vector.tensor_tensor(out=f_cell[:], in0=f_back[:], in1=cell_rows[c][:, :, cols], op=ALU.mult)
-            return f_cell
-
-        def finish_c(c, half, cand_i, f_cell, c_sb):
-            cols = slice(half * P, (half + 1) * P)
-            ci_back = turn_back(cand_i)
-            nc.vector.tensor_tensor(out=c_sb[:, :, cols], in0=ci_back[:], in1=f_cell[:], op=ALU.add)
-
         def store(c, h_sb, c_sb):
             rows = slice(c * CHUNK, (c + 1) * CHUNK)
             nc.sync.dma_start(out=out_0[rows, :].rearrange("(p t) h -> p t h", t=ROW_TILES), in_=h_sb[:])
             nc.sync.dma_start(out=out_1[rows, :].rearrange("(p t) h -> p t h", t=ROW_TILES), in_=c_sb[:])
-
-        for number in range(PASSES):
-            quantise_z_pass(turn_z_pass(number, (1,)))
 
         bias_rows_f32 = const.tile([P, P], F32)
         nc.vector.tensor_copy(out=bias_rows_f32[:], in_=bias_rows[:])
@@ -202,35 +231,62 @@ def tile_quest_pa_t_kernel(
         nc.tensor.transpose(bias_ps[:], bias_rows_f32[:], ident[:])
         bias_sb = const.tile([P, HALVES * len(GATES)], F32)
         nc.vector.tensor_copy(out=bias_sb[:], in_=bias_ps[:, 0 : HALVES * len(GATES)])
+        bias_f_ps = psum.tile([P, HALVES, P], F32, tag="bank")
+        for half in range(HALVES):
+            row = HALVES * GATES.index("f") + half
+            nc.tensor.matmul(
+                out=bias_f_ps[:, half, :],
+                lhsT=ident[:, row : row + 1].to_broadcast([P, P]),
+                rhs=bias_rows_f32[:],
+                start=True,
+                stop=True,
+            )
+        bias_f = const.tile([P, HID], F32)
+        nc.vector.tensor_copy(out=bias_f[:], in_=bias_f_ps[:].rearrange("p e j -> p (e j)"))
 
-        w_codes = const.tile([P, len(GATES), PASSES, HID], U32, align_bytes=64)
-        w_scales = const.tile([P, len(GATES), PASSES, HID], U8, align_bytes=64)
-        for gi, gate in enumerate(GATES):
-            w_grouped = [turn_pass(w_rows[gate], HALVES, g, (0,) if g == 1 else ()) for g in range(PASSES)]
-            for g in range(PASSES):
-                quantise(w_grouped[g], w_codes[:, gi, g, :], w_scales[:, gi, g, :])
+        for m in range(2):
+            turn_z_pair(m, True)
+        quantise_z(0)
+        for n, (gate, half) in enumerate(w_for_round_0):
+            prepare_w(gate, half, n % 2 == 1)
 
+        f_cells = []
+        next_pair = 2
         before = None
         for s in range(N_ROUNDS + 1):
-            if s < N_ROUNDS:
+            running = s < N_ROUNDS
+            if running:
                 c, half = divmod(s, HALVES)
                 if half == 0:
                     h_sb = out_pool.tile([P, ROW_TILES, HID], F32)
                     c_sb = out_pool.tile([P, ROW_TILES, HID], F32)
-                f_gate, cand_i, h_turned = compute_gates(c, half)
+                cand_i, h_turned = turned_gates(c, half)
+                if half == 0:
+                    f_gate = forget_sums(c)
             if before is not None:
-                f_cell = finish_h_and_f(before["c"], before["half"], before["f_gate"], before["h_turned"], before["h_sb"])
-            fresh = [
-                turn_z_pass(number, ())
-                for number in range(len(z_codes), min(s + AHEAD, N_Z_PASSES - 1) + 1)
-            ]
+                cols = slice(before["half"] * P, (before["half"] + 1) * P)
+                h_back = turn_back(before["h_turned"])
+                nc.scalar.copy(out=before["h_sb"][:, :, cols], in_=h_back[:])
+                ci_back = turn_back(before["cand_i"])
+            if running and half == 0:
+                nc.scalar.activation(out=f_gate[:], in_=f_gate[:], func=ACT.Sigmoid)
+            if running and half == 1:
+                f_cell = gate_pool.tile([P, ROW_TILES, HID], F32)
+                nc.vector.tensor_tensor(out=f_cell[:], in0=f_gate[:], in1=cell_rows[c][:], op=ALU.mult)
+                f_cells.append(f_cell)
             if before is not None:
-                finish_c(before["c"], before["half"], before["cand_i"], f_cell, before["c_sb"])
-            for grouped in fresh:
-                quantise_z_pass(grouped)
-            if before is not None and before["half"] == HALVES - 1:
-                store(before["c"], before["h_sb"], before["c_sb"])
-            before = {
-                "c": c, "half": half, "f_gate": f_gate, "cand_i": cand_i, "h_turned": h_turned,
-                "h_sb": h_sb, "c_sb": c_sb,
-            }
+                nc.vector.tensor_tensor(
+                    out=before["c_sb"][:, :, cols], in0=ci_back[:], in1=f_cells[before["c"]][:, :, cols], op=ALU.add
+                )
+                if before["half"] == HALVES - 1:
+                    store(before["c"], before["h_sb"], before["c_sb"])
+            if s == 0:
+                for gate, w_half in w_for_round_1:
+                    prepare_w(gate, w_half, False)
+            pairs_end = max(next_pair, min(s + AHEAD, N_PAIRS - 1) + 1)
+            for m in range(next_pair, pairs_end):
+                turn_z_pair(m, False)
+                if m % 2 == 1:
+                    quantise_z(m // 2)
+            next_pair = pairs_end
+            before = {"c": c, "half": half, "cand_i": cand_i, "h_turned": h_turned, "h_sb": h_sb, "c_sb": c_sb}

@@ -18,6 +18,7 @@ K = 1024
 N_X = 768
 K_PASS = P * PACK
 PASSES = K // K_PASS
+PASS_WORDS = K_PASS // 2
 BATCH = 4096
 CHUNK = 512
 ROW_TILES = CHUNK // P
@@ -25,11 +26,10 @@ N_CHUNKS = BATCH // CHUNK
 HID = 256
 HALVES = HID // P
 N_ROUNDS = N_CHUNKS * HALVES
-N_PAIRS = N_CHUNKS * 2
+N_Z_PASSES = N_CHUNKS * PASSES
 AHEAD = 3
 GATES = ("cand", "i", "o", "f")
-TURNED_GATES = ("cand", "i", "o")
-GATE_FUNC = {"cand": ACT.Tanh, "i": ACT.Sigmoid, "o": ACT.Sigmoid}
+GATE_FUNC = {"cand": ACT.Tanh, "i": ACT.Sigmoid, "o": ACT.Sigmoid, "f": ACT.Sigmoid}
 
 FLOPS = 2 * BATCH * K * 4 * HID
 
@@ -44,10 +44,10 @@ def tile_quest_pa_t_kernel(
     with ExitStack() as stack:
         stack.enter_context(tc.manual_schedule())
         const = stack.enter_context(tc.tile_pool(name="const", bufs=1))
-        w_pool = stack.enter_context(tc.tile_pool(name="w_raw", bufs=len(GATES) * HALVES))
+        w_pool = stack.enter_context(tc.tile_pool(name="w_raw", bufs=len(GATES)))
         in_pool = stack.enter_context(tc.tile_pool(name="inputs", bufs=N_CHUNKS))
-        grouped_pool = stack.enter_context(tc.tile_pool(name="grouped", bufs=2))
-        codes_pool = stack.enter_context(tc.tile_pool(name="codes", bufs=3))
+        grouped_pool = stack.enter_context(tc.tile_pool(name="grouped", bufs=3))
+        codes_pool = stack.enter_context(tc.tile_pool(name="codes", bufs=PASSES + AHEAD))
         gate_pool = stack.enter_context(tc.tile_pool(name="gates", bufs=2))
         out_pool = stack.enter_context(tc.tile_pool(name="outs", bufs=3))
         psum = stack.enter_context(tc.psum_pool(name="psum", bufs=PSUM_BANKS))
@@ -62,7 +62,6 @@ def tile_quest_pa_t_kernel(
 
         z_rows = []
         cell_rows = []
-        w_rows = {}
 
         def load_z(c):
             rows = slice(c * CHUNK, (c + 1) * CHUNK)
@@ -83,16 +82,12 @@ def tile_quest_pa_t_kernel(
             )
             cell_rows.append(cell_sb)
 
-        def load_w(gate, half):
-            w_sb = w_pool.tile([P, K], BF16)
-            nc.sync.dma_start(out=w_sb[:], in_=weights[gate][half * P : (half + 1) * P, :])
-            w_rows[(gate, half)] = w_sb
-
-        w_for_round_0 = [(gate, 0) for gate in TURNED_GATES] + [("f", 0), ("f", 1)]
-        w_for_round_1 = [(gate, 1) for gate in TURNED_GATES]
         load_z(0)
-        for gate, half in w_for_round_0 + w_for_round_1:
-            load_w(gate, half)
+        w_rows = {}
+        for gate in GATES:
+            w_sb = w_pool.tile([P, HALVES, K], BF16)
+            nc.sync.dma_start(out=w_sb[:], in_=weights[gate].rearrange("(e p) k -> p e k", p=P))
+            w_rows[gate] = w_sb
         for c in range(1, N_CHUNKS):
             load_z(c)
             load_cell(c - 1)
@@ -105,72 +100,55 @@ def tile_quest_pa_t_kernel(
         nc.vector.memset(warm_in[:], 0.0)
         nc.scalar.activation(out=warm_out[:], in_=warm_in[:], func=ACT.Sigmoid)
 
-        def words_view(grouped):
-            return grouped[:].bitcast(F32).rearrange("p (g j u) -> p g j u", g=PASSES, u=2)
-
-        def turn_rows(rows, dst_words, on_scalar):
-            bank = psum.tile([P, PASSES, 2, P], F32, tag="bank")
-            words = rows.bitcast(F32)
-            for g in range(PASSES):
+        def turn_pass(rows_sb, n_row_tiles, g, pairs_on_scalar):
+            grouped = grouped_pool.tile([P, n_row_tiles * P * PACK], BF16, align_bytes=64)
+            grouped_words = grouped[:].bitcast(F32).rearrange("p (j u) -> p j u", u=2)
+            for pair in range(n_row_tiles // 2):
+                turned = psum.tile([P, 2, 2 * P], F32, tag="bank")
                 for u in range(2):
-                    first = (2 * g + u) * P
-                    nc.tensor.transpose(bank[:, g, u, :], words[:, first : first + P], ident[:])
-            src = bank[:].rearrange("p g u j -> p g j u")
-            if on_scalar:
-                nc.scalar.copy(out=dst_words, in_=src)
-            else:
-                nc.vector.tensor_copy(out=dst_words, in_=src)
+                    first = PASS_WORDS * g + P * u
+                    for r in range(2):
+                        words = rows_sb[:, 2 * pair + r, :].bitcast(F32)
+                        nc.tensor.transpose(
+                            turned[:, u, r * P : (r + 1) * P], words[:, first : first + P], ident[:]
+                        )
+                dst = grouped_words[:, 2 * pair * P : 2 * (pair + 1) * P, :]
+                src = turned[:].rearrange("p u j -> p j u")
+                if pair in pairs_on_scalar:
+                    nc.scalar.copy(out=dst, in_=src)
+                else:
+                    nc.vector.tensor_copy(out=dst, in_=src)
+            return grouped
 
-        def quantise(grouped, n_cols, g, codes, scales):
-            values = grouped[:, g * n_cols * PACK : (g + 1) * n_cols * PACK]
-            nc.vector.quantize_mx(out=codes.bitcast(FP8X4), scales=scales, in_=values)
+        def quantise(grouped, codes, scales):
+            nc.vector.quantize_mx(out=codes.bitcast(FP8X4), scales=scales, in_=grouped[:])
 
-        w_codes = const.tile([P, len(GATES), PASSES, HID], U32, align_bytes=64)
-        w_scales = const.tile([P, len(GATES), PASSES, HID], U8, align_bytes=64)
-
-        def prepare_w(gate, half, on_scalar):
-            w_grouped = grouped_pool.tile([P, PASSES * P * PACK], BF16, align_bytes=64)
-            turn_rows(w_rows[(gate, half)][:], words_view(w_grouped), on_scalar)
-            gi = GATES.index(gate)
-            cols = slice(half * P, (half + 1) * P)
-            for g in range(PASSES):
-                quantise(w_grouped, P, g, w_codes[:, gi, g, cols], w_scales[:, gi, g, cols])
-
-        z_grouped = []
         z_codes = []
         z_scales = []
 
-        def turn_z_pair(m, second_on_scalar):
-            c, part = divmod(m, 2)
-            if part == 0:
-                grouped = grouped_pool.tile([P, PASSES * CHUNK * PACK], BF16, align_bytes=64)
-                z_grouped.append(grouped)
-            for r in range(2):
-                t = 2 * part + r
-                dst_words = words_view(z_grouped[c])[:, :, t * P : (t + 1) * P, :]
-                turn_rows(z_rows[c][:, t, :], dst_words, second_on_scalar and r == 1)
+        def turn_z_pass(number, pairs_on_scalar):
+            c, g = divmod(number, PASSES)
+            return turn_pass(z_rows[c], ROW_TILES, g, pairs_on_scalar)
 
-        def quantise_z(c):
-            codes = codes_pool.tile([P, PASSES, CHUNK], U32, align_bytes=64)
-            scales = codes_pool.tile([P, PASSES, CHUNK], U8, align_bytes=64)
-            for g in range(PASSES):
-                quantise(z_grouped[c], CHUNK, g, codes[:, g, :], scales[:, g, :])
+        def quantise_z_pass(grouped):
+            codes = codes_pool.tile([P, CHUNK], U32, align_bytes=64)
+            scales = codes_pool.tile([P, CHUNK], U8, align_bytes=64)
+            quantise(grouped, codes[:], scales[:])
             z_codes.append(codes)
             z_scales.append(scales)
 
-        def turned_gates(c, half):
+        def compute_gates(c, half):
             cols = slice(half * P, (half + 1) * P)
             val = {}
-            for gate in TURNED_GATES:
-                gi = GATES.index(gate)
+            for gi, gate in enumerate(GATES):
                 acc = psum.tile([P, CHUNK], F32, tag="bank")
                 for g in range(PASSES):
                     nc.tensor.matmul_mx(
                         out=acc[:],
                         lhsT=w_codes[:, gi, g, cols].bitcast(FP8X4),
                         lhsT_scale=w_scales[:, gi, g, cols],
-                        rhs=z_codes[c][:, g, :].bitcast(FP8X4),
-                        rhs_scale=z_scales[c][:, g, :],
+                        rhs=z_codes[PASSES * c + g][:].bitcast(FP8X4),
+                        rhs_scale=z_scales[PASSES * c + g][:],
                         start=(g == 0),
                         stop=(g == PASSES - 1),
                     )
@@ -185,34 +163,10 @@ def tile_quest_pa_t_kernel(
                     nc.scalar.activation(out=tanh_cand[:], in_=val["cand"][:], func=ACT.Tanh)
                     cand_i = gate_pool.tile([P, CHUNK], F32)
                     nc.gpsimd.tensor_tensor(out=cand_i[:], in0=val["cand"][:], in1=val["i"][:], op=ALU.mult)
-            h_turned = gate_pool.tile([P, CHUNK], F32)
-            nc.gpsimd.tensor_tensor(out=h_turned[:], in0=val["o"][:], in1=tanh_cand[:], op=ALU.mult)
-            return cand_i, h_turned
-
-        def forget_sums(c):
-            gi = GATES.index("f")
-            f_gate = gate_pool.tile([P, ROW_TILES, HID], F32)
-            for part in range(2):
-                acc = psum.tile([P, 2, HID], F32, tag="bank")
-                for r in range(2):
-                    cols = slice((2 * part + r) * P, (2 * part + r + 1) * P)
-                    for g in range(PASSES):
-                        nc.tensor.matmul_mx(
-                            out=acc[:, r, :],
-                            lhsT=z_codes[c][:, g, cols].bitcast(FP8X4),
-                            lhsT_scale=z_scales[c][:, g, cols],
-                            rhs=w_codes[:, gi, g, :].bitcast(FP8X4),
-                            rhs_scale=w_scales[:, gi, g, :],
-                            start=(g == 0),
-                            stop=(g == PASSES - 1),
-                        )
-                nc.vector.tensor_tensor(
-                    out=f_gate[:, 2 * part : 2 * part + 2, :],
-                    in0=acc[:],
-                    in1=bias_f[:].unsqueeze(1).to_broadcast([P, 2, HID]),
-                    op=ALU.add,
-                )
-            return f_gate
+                if gate == "o":
+                    h_turned = gate_pool.tile([P, CHUNK], F32)
+                    nc.gpsimd.tensor_tensor(out=h_turned[:], in0=val["o"][:], in1=tanh_cand[:], op=ALU.mult)
+            return val["f"], cand_i, h_turned
 
         def turn_back(src):
             back = psum.tile([P, ROW_TILES, P], F32, tag="bank")
@@ -220,10 +174,30 @@ def tile_quest_pa_t_kernel(
                 nc.tensor.transpose(back[:, t, :], src[:, t * P : (t + 1) * P], ident[:])
             return back
 
+        def finish_h_and_f(c, half, f_gate, h_turned, h_sb):
+            cols = slice(half * P, (half + 1) * P)
+            h_back = turn_back(h_turned)
+            f_back = turn_back(f_gate)
+            if half == 0:
+                nc.vector.tensor_copy(out=h_sb[:, :, cols], in_=h_back[:])
+            else:
+                nc.scalar.copy(out=h_sb[:, :, cols], in_=h_back[:])
+            f_cell = out_pool.tile([P, ROW_TILES, P], F32)
+            nc.vector.tensor_tensor(out=f_cell[:], in0=f_back[:], in1=cell_rows[c][:, :, cols], op=ALU.mult)
+            return f_cell
+
+        def finish_c(c, half, cand_i, f_cell, c_sb):
+            cols = slice(half * P, (half + 1) * P)
+            ci_back = turn_back(cand_i)
+            nc.vector.tensor_tensor(out=c_sb[:, :, cols], in0=ci_back[:], in1=f_cell[:], op=ALU.add)
+
         def store(c, h_sb, c_sb):
             rows = slice(c * CHUNK, (c + 1) * CHUNK)
             nc.sync.dma_start(out=out_0[rows, :].rearrange("(p t) h -> p t h", t=ROW_TILES), in_=h_sb[:])
             nc.sync.dma_start(out=out_1[rows, :].rearrange("(p t) h -> p t h", t=ROW_TILES), in_=c_sb[:])
+
+        for number in range(PASSES):
+            quantise_z_pass(turn_z_pass(number, (1,)))
 
         bias_rows_f32 = const.tile([P, P], F32)
         nc.vector.tensor_copy(out=bias_rows_f32[:], in_=bias_rows[:])
@@ -231,62 +205,35 @@ def tile_quest_pa_t_kernel(
         nc.tensor.transpose(bias_ps[:], bias_rows_f32[:], ident[:])
         bias_sb = const.tile([P, HALVES * len(GATES)], F32)
         nc.vector.tensor_copy(out=bias_sb[:], in_=bias_ps[:, 0 : HALVES * len(GATES)])
-        bias_f_ps = psum.tile([P, HALVES, P], F32, tag="bank")
-        for half in range(HALVES):
-            row = HALVES * GATES.index("f") + half
-            nc.tensor.matmul(
-                out=bias_f_ps[:, half, :],
-                lhsT=ident[:, row : row + 1].to_broadcast([P, P]),
-                rhs=bias_rows_f32[:],
-                start=True,
-                stop=True,
-            )
-        bias_f = const.tile([P, HID], F32)
-        nc.vector.tensor_copy(out=bias_f[:], in_=bias_f_ps[:].rearrange("p e j -> p (e j)"))
 
-        for m in range(2):
-            turn_z_pair(m, True)
-        quantise_z(0)
-        for n, (gate, half) in enumerate(w_for_round_0):
-            prepare_w(gate, half, n % 2 == 1)
+        w_codes = const.tile([P, len(GATES), PASSES, HID], U32, align_bytes=64)
+        w_scales = const.tile([P, len(GATES), PASSES, HID], U8, align_bytes=64)
+        for gi, gate in enumerate(GATES):
+            w_grouped = [turn_pass(w_rows[gate], HALVES, g, (0,)) for g in range(PASSES)]
+            for g in range(PASSES):
+                quantise(w_grouped[g], w_codes[:, gi, g, :], w_scales[:, gi, g, :])
 
-        f_cells = []
-        next_pair = 2
         before = None
         for s in range(N_ROUNDS + 1):
-            running = s < N_ROUNDS
-            if running:
+            if s < N_ROUNDS:
                 c, half = divmod(s, HALVES)
                 if half == 0:
                     h_sb = out_pool.tile([P, ROW_TILES, HID], F32)
                     c_sb = out_pool.tile([P, ROW_TILES, HID], F32)
-                cand_i, h_turned = turned_gates(c, half)
-                if half == 0:
-                    f_gate = forget_sums(c)
+                f_gate, cand_i, h_turned = compute_gates(c, half)
             if before is not None:
-                cols = slice(before["half"] * P, (before["half"] + 1) * P)
-                h_back = turn_back(before["h_turned"])
-                nc.scalar.copy(out=before["h_sb"][:, :, cols], in_=h_back[:])
-                ci_back = turn_back(before["cand_i"])
-            if running and half == 0:
-                nc.scalar.activation(out=f_gate[:], in_=f_gate[:], func=ACT.Sigmoid)
-            if running and half == 1:
-                f_cell = gate_pool.tile([P, ROW_TILES, HID], F32)
-                nc.vector.tensor_tensor(out=f_cell[:], in0=f_gate[:], in1=cell_rows[c][:], op=ALU.mult)
-                f_cells.append(f_cell)
+                f_cell = finish_h_and_f(before["c"], before["half"], before["f_gate"], before["h_turned"], before["h_sb"])
+            fresh = [
+                turn_z_pass(number, ())
+                for number in range(len(z_codes), min(s + AHEAD, N_Z_PASSES - 1) + 1)
+            ]
             if before is not None:
-                nc.vector.tensor_tensor(
-                    out=before["c_sb"][:, :, cols], in0=ci_back[:], in1=f_cells[before["c"]][:, :, cols], op=ALU.add
-                )
-                if before["half"] == HALVES - 1:
-                    store(before["c"], before["h_sb"], before["c_sb"])
-            if s == 0:
-                for gate, w_half in w_for_round_1:
-                    prepare_w(gate, w_half, False)
-            pairs_end = max(next_pair, min(s + AHEAD, N_PAIRS - 1) + 1)
-            for m in range(next_pair, pairs_end):
-                turn_z_pair(m, False)
-                if m % 2 == 1:
-                    quantise_z(m // 2)
-            next_pair = pairs_end
-            before = {"c": c, "half": half, "cand_i": cand_i, "h_turned": h_turned, "h_sb": h_sb, "c_sb": c_sb}
+                finish_c(before["c"], before["half"], before["cand_i"], f_cell, before["c_sb"])
+            for grouped in fresh:
+                quantise_z_pass(grouped)
+            if before is not None and before["half"] == HALVES - 1:
+                store(before["c"], before["h_sb"], before["c_sb"])
+            before = {
+                "c": c, "half": half, "f_gate": f_gate, "cand_i": cand_i, "h_turned": h_turned,
+                "h_sb": h_sb, "c_sb": c_sb,
+            }

@@ -12,7 +12,6 @@ ACT = mybir.ActivationFunctionType
 ALU = mybir.AluOpType
 
 P = 128
-PSUM_BANKS = 8
 PACK = 4
 K = 1024
 N_X = 768
@@ -25,40 +24,38 @@ ROW_TILES = CHUNK // P
 N_CHUNKS = BATCH // CHUNK
 HID = 256
 HALVES = HID // P
-N_ROUNDS = N_CHUNKS * HALVES
-N_Z_PASSES = N_CHUNKS * PASSES
-AHEAD = 3
 GATES = ("cand", "i", "o", "f")
+LAST_GATES = ("cand", "i", "f", "o")
 GATE_FUNC = {"cand": ACT.Tanh, "i": ACT.Sigmoid, "o": ACT.Sigmoid, "f": ACT.Sigmoid}
-
 FLOPS = 2 * BATCH * K * 4 * HID
+AHEAD = 3
+TAIL_PIECES = ((0, 4),)
+V_TAIL = 0
+W1_ENG = "VSVS"
+Z_ENG = {2: "SS", 3: "SV"}
+N_ROUNDS = N_CHUNKS * HALVES
+N_PIECES = N_CHUNKS * PASSES
 
 
-def tile_quest_pa_t_kernel(
-    tc, X, hidden1, cell1, Wf1, bf1, Wi1, bi1, Wc1, bc1, Wo1, bo1, out_0, out_1
-):
+def tile_quest_pa_t_kernel(tc, X, hidden1, cell1, Wf1, bf1, Wi1, bi1, Wc1, bc1, Wo1, bo1, out_0, out_1):
     nc = tc.nc
     weights = {"f": Wf1, "i": Wi1, "cand": Wc1, "o": Wo1}
     biases = {"f": bf1, "i": bi1, "cand": bc1, "o": bo1}
-
     with ExitStack() as stack:
         stack.enter_context(tc.manual_schedule())
         const = stack.enter_context(tc.tile_pool(name="const", bufs=1))
-        w_pool = stack.enter_context(tc.tile_pool(name="w_raw", bufs=len(GATES)))
+        w_pool = stack.enter_context(tc.tile_pool(name="w_raw", bufs=len(GATES) * HALVES))
         in_pool = stack.enter_context(tc.tile_pool(name="inputs", bufs=N_CHUNKS))
         grouped_pool = stack.enter_context(tc.tile_pool(name="grouped", bufs=3))
         codes_pool = stack.enter_context(tc.tile_pool(name="codes", bufs=PASSES + AHEAD))
         gate_pool = stack.enter_context(tc.tile_pool(name="gates", bufs=2))
         out_pool = stack.enter_context(tc.tile_pool(name="outs", bufs=3))
-        psum = stack.enter_context(tc.psum_pool(name="psum", bufs=PSUM_BANKS))
+        psum = stack.enter_context(tc.psum_pool(name="psum", bufs=8))
 
         bias_rows = const.tile([P, P], BF16)
         nc.vector.memset(bias_rows[:], 0.0)
         for gi, gate in enumerate(GATES):
-            nc.scalar.dma_start(
-                out=bias_rows[HALVES * gi : HALVES * (gi + 1), :],
-                in_=biases[gate].rearrange("(e p) -> e p", p=P),
-            )
+            nc.scalar.dma_start(out=bias_rows[HALVES * gi : HALVES * (gi + 1), :], in_=biases[gate].rearrange("(e p) -> e p", p=P))
 
         z_rows = []
         cell_rows = []
@@ -66,28 +63,30 @@ def tile_quest_pa_t_kernel(
         def load_z(c):
             rows = slice(c * CHUNK, (c + 1) * CHUNK)
             z_sb = in_pool.tile([P, ROW_TILES, K], BF16)
-            nc.sync.dma_start(
-                out=z_sb[:, :, 0:N_X], in_=X[rows, :].rearrange("(p t) k -> p t k", t=ROW_TILES)
-            )
-            nc.sync.dma_start(
-                out=z_sb[:, :, N_X:K], in_=hidden1[rows, :].rearrange("(p t) k -> p t k", t=ROW_TILES)
-            )
+            nc.sync.dma_start(out=z_sb[:, :, 0:N_X], in_=X[rows, :].rearrange("(p t) k -> p t k", t=ROW_TILES))
+            nc.sync.dma_start(out=z_sb[:, :, N_X:K], in_=hidden1[rows, :].rearrange("(p t) k -> p t k", t=ROW_TILES))
             z_rows.append(z_sb)
 
         def load_cell(c):
             rows = slice(c * CHUNK, (c + 1) * CHUNK)
             cell_sb = in_pool.tile([P, ROW_TILES, HID], BF16)
-            nc.sync.dma_start(
-                out=cell_sb[:], in_=cell1[rows, :].rearrange("(p t) h -> p t h", t=ROW_TILES)
-            )
+            nc.sync.dma_start(out=cell_sb[:], in_=cell1[rows, :].rearrange("(p t) h -> p t h", t=ROW_TILES))
             cell_rows.append(cell_sb)
 
-        load_z(0)
+
         w_rows = {}
+
+        def load_w(gate, half):
+            w_sb = w_pool.tile([P, K], BF16)
+            nc.sync.dma_start(out=w_sb[:], in_=weights[gate][half * P : (half + 1) * P, :])
+            w_rows[gate, half] = w_sb
+
+        load_w(GATES[0], 0)
+        load_z(0)
+        for gate in GATES[1:]:
+            load_w(gate, 0)
         for gate in GATES:
-            w_sb = w_pool.tile([P, HALVES, K], BF16)
-            nc.sync.dma_start(out=w_sb[:], in_=weights[gate].rearrange("(e p) k -> p e k", p=P))
-            w_rows[gate] = w_sb
+            load_w(gate, 1)
         for c in range(1, N_CHUNKS):
             load_z(c)
             load_cell(c - 1)
@@ -100,105 +99,6 @@ def tile_quest_pa_t_kernel(
         nc.vector.memset(warm_in[:], 0.0)
         nc.scalar.activation(out=warm_out[:], in_=warm_in[:], func=ACT.Sigmoid)
 
-        def turn_pass(rows_sb, n_row_tiles, g, pairs_on_scalar):
-            grouped = grouped_pool.tile([P, n_row_tiles * P * PACK], BF16, align_bytes=64)
-            grouped_words = grouped[:].bitcast(F32).rearrange("p (j u) -> p j u", u=2)
-            for pair in range(n_row_tiles // 2):
-                turned = psum.tile([P, 2, 2 * P], F32, tag="bank")
-                for u in range(2):
-                    first = PASS_WORDS * g + P * u
-                    for r in range(2):
-                        words = rows_sb[:, 2 * pair + r, :].bitcast(F32)
-                        nc.tensor.transpose(
-                            turned[:, u, r * P : (r + 1) * P], words[:, first : first + P], ident[:]
-                        )
-                dst = grouped_words[:, 2 * pair * P : 2 * (pair + 1) * P, :]
-                src = turned[:].rearrange("p u j -> p j u")
-                if pair in pairs_on_scalar:
-                    nc.scalar.copy(out=dst, in_=src)
-                else:
-                    nc.vector.tensor_copy(out=dst, in_=src)
-            return grouped
-
-        def quantise(grouped, codes, scales):
-            nc.vector.quantize_mx(out=codes.bitcast(FP8X4), scales=scales, in_=grouped[:])
-
-        z_codes = []
-        z_scales = []
-
-        def turn_z_pass(number, pairs_on_scalar):
-            c, g = divmod(number, PASSES)
-            return turn_pass(z_rows[c], ROW_TILES, g, pairs_on_scalar)
-
-        def quantise_z_pass(grouped):
-            codes = codes_pool.tile([P, CHUNK], U32, align_bytes=64)
-            scales = codes_pool.tile([P, CHUNK], U8, align_bytes=64)
-            quantise(grouped, codes[:], scales[:])
-            z_codes.append(codes)
-            z_scales.append(scales)
-
-        def compute_gates(c, half):
-            cols = slice(half * P, (half + 1) * P)
-            val = {}
-            for gi, gate in enumerate(GATES):
-                acc = psum.tile([P, CHUNK], F32, tag="bank")
-                for g in range(PASSES):
-                    nc.tensor.matmul_mx(
-                        out=acc[:],
-                        lhsT=w_codes[:, gi, g, cols].bitcast(FP8X4),
-                        lhsT_scale=w_scales[:, gi, g, cols],
-                        rhs=z_codes[PASSES * c + g][:].bitcast(FP8X4),
-                        rhs_scale=z_scales[PASSES * c + g][:],
-                        start=(g == 0),
-                        stop=(g == PASSES - 1),
-                    )
-                gate_sb = gate_pool.tile([P, CHUNK], F32, tag="gate_" + gate)
-                col = HALVES * gi + half
-                nc.scalar.activation(
-                    out=gate_sb[:], in_=acc[:], func=GATE_FUNC[gate], bias=bias_sb[:, col : col + 1], scale=1.0
-                )
-                val[gate] = gate_sb
-                if gate == "i":
-                    tanh_cand = gate_pool.tile([P, CHUNK], F32)
-                    nc.scalar.activation(out=tanh_cand[:], in_=val["cand"][:], func=ACT.Tanh)
-                    cand_i = gate_pool.tile([P, CHUNK], F32)
-                    nc.gpsimd.tensor_tensor(out=cand_i[:], in0=val["cand"][:], in1=val["i"][:], op=ALU.mult)
-                if gate == "o":
-                    h_turned = gate_pool.tile([P, CHUNK], F32)
-                    nc.gpsimd.tensor_tensor(out=h_turned[:], in0=val["o"][:], in1=tanh_cand[:], op=ALU.mult)
-            return val["f"], cand_i, h_turned
-
-        def turn_back(src):
-            back = psum.tile([P, ROW_TILES, P], F32, tag="bank")
-            for t in range(ROW_TILES):
-                nc.tensor.transpose(back[:, t, :], src[:, t * P : (t + 1) * P], ident[:])
-            return back
-
-        def finish_h_and_f(c, half, f_gate, h_turned, h_sb):
-            cols = slice(half * P, (half + 1) * P)
-            h_back = turn_back(h_turned)
-            f_back = turn_back(f_gate)
-            if half == 0:
-                nc.vector.tensor_copy(out=h_sb[:, :, cols], in_=h_back[:])
-            else:
-                nc.scalar.copy(out=h_sb[:, :, cols], in_=h_back[:])
-            f_cell = out_pool.tile([P, ROW_TILES, P], F32)
-            nc.vector.tensor_tensor(out=f_cell[:], in0=f_back[:], in1=cell_rows[c][:, :, cols], op=ALU.mult)
-            return f_cell
-
-        def finish_c(c, half, cand_i, f_cell, c_sb):
-            cols = slice(half * P, (half + 1) * P)
-            ci_back = turn_back(cand_i)
-            nc.vector.tensor_tensor(out=c_sb[:, :, cols], in0=ci_back[:], in1=f_cell[:], op=ALU.add)
-
-        def store(c, h_sb, c_sb):
-            rows = slice(c * CHUNK, (c + 1) * CHUNK)
-            nc.sync.dma_start(out=out_0[rows, :].rearrange("(p t) h -> p t h", t=ROW_TILES), in_=h_sb[:])
-            nc.sync.dma_start(out=out_1[rows, :].rearrange("(p t) h -> p t h", t=ROW_TILES), in_=c_sb[:])
-
-        for number in range(PASSES):
-            quantise_z_pass(turn_z_pass(number, (1,)))
-
         bias_rows_f32 = const.tile([P, P], F32)
         nc.vector.tensor_copy(out=bias_rows_f32[:], in_=bias_rows[:])
         bias_ps = psum.tile([P, P], F32, tag="bank")
@@ -206,34 +106,171 @@ def tile_quest_pa_t_kernel(
         bias_sb = const.tile([P, HALVES * len(GATES)], F32)
         nc.vector.tensor_copy(out=bias_sb[:], in_=bias_ps[:, 0 : HALVES * len(GATES)])
 
-        w_codes = const.tile([P, len(GATES), PASSES, HID], U32, align_bytes=64)
-        w_scales = const.tile([P, len(GATES), PASSES, HID], U8, align_bytes=64)
-        for gi, gate in enumerate(GATES):
-            w_grouped = [turn_pass(w_rows[gate], HALVES, g, (0,)) for g in range(PASSES)]
-            for g in range(PASSES):
-                quantise(w_grouped[g], w_codes[:, gi, g, :], w_scales[:, gi, g, :])
+        def copy_out(dst, src, engine):
+            if engine == "S":
+                nc.scalar.copy(out=dst, in_=src)
+            else:
+                nc.vector.tensor_copy(out=dst, in_=src)
 
+        z_codes = []
+        z_scales = []
+
+        def turn_z(number, engines):
+            c, g = divmod(number, PASSES)
+            grouped = grouped_pool.tile([P, CHUNK * PACK], BF16, align_bytes=64)
+            words = grouped[:].bitcast(F32).rearrange("p (j u) -> p j u", u=2)
+            for pair in range(ROW_TILES // 2):
+                turned = psum.tile([P, 2, 2 * P], F32, tag="bank")
+                for u in range(2):
+                    first = PASS_WORDS * g + P * u
+                    for r in range(2):
+                        src_words = z_rows[c][:, 2 * pair + r, :].bitcast(F32)
+                        nc.tensor.transpose(turned[:, u, r * P : (r + 1) * P], src_words[:, first : first + P], ident[:])
+                copy_out(words[:, 2 * pair * P : 2 * (pair + 1) * P, :], turned[:].rearrange("p u j -> p j u"), engines[pair])
+            return grouped
+
+        def quantise_z(grouped):
+            codes = codes_pool.tile([P, CHUNK], U32, align_bytes=64)
+            scales = codes_pool.tile([P, CHUNK], U8, align_bytes=64)
+            nc.vector.quantize_mx(out=codes[:].bitcast(FP8X4), scales=scales[:], in_=grouped[:])
+            z_codes.append(codes)
+            z_scales.append(scales)
+
+        w_codes = const.tile([P, len(GATES), HALVES, PASSES, P], U32, align_bytes=64)
+        w_scales = const.tile([P, len(GATES), HALVES, PASSES, P], U8, align_bytes=64)
+
+        def turn_w(gate, half, engine):
+            grouped_w = grouped_pool.tile([P, PASSES * P * PACK], BF16, align_bytes=64, bufs=4)
+            turned = psum.tile([P, PASSES, 2, P], F32, tag="bank")
+            src_words = w_rows[gate, half][:].bitcast(F32)
+            for g in range(PASSES):
+                for u in range(2):
+                    first = PASS_WORDS * g + P * u
+                    nc.tensor.transpose(turned[:, g, u, :], src_words[:, first : first + P], ident[:])
+            copy_out(grouped_w[:].bitcast(F32).rearrange("p (g j u) -> p g j u", g=PASSES, u=2), turned[:].rearrange("p g u j -> p g j u"), engine)
+            return grouped_w
+
+        def quantise_w(gate, half, grouped_w):
+            gi = GATES.index(gate)
+            nc.vector.quantize_mx(
+                out=w_codes[:, gi, half, :, :].rearrange("p g h -> p (g h)").bitcast(FP8X4),
+                scales=w_scales[:, gi, half, :, :].rearrange("p g h -> p (g h)"), in_=grouped_w[:])
+
+        def compute_gates(r):
+            c, half, t0, nt = r["c"], r["half"], r["t0"], r["nt"]
+            n = nt * P
+            batch = slice(t0 * P, t0 * P + n)
+            for gate in r["order"]:
+                gi = GATES.index(gate)
+                acc = psum.tile([P, n], F32, tag="bank")
+                for g in range(PASSES):
+                    nc.tensor.matmul_mx(out=acc[:], lhsT=w_codes[:, gi, half, g, :].bitcast(FP8X4), lhsT_scale=w_scales[:, gi, half, g, :],
+                                        rhs=z_codes[PASSES * c + g][:, batch].bitcast(FP8X4), rhs_scale=z_scales[PASSES * c + g][:, batch],
+                                        start=(g == 0), stop=(g == PASSES - 1))
+                gate_sb = gate_pool.tile([P, n], F32, tag="gate_" + gate)
+                col = HALVES * gi + half
+                nc.scalar.activation(out=gate_sb[:], in_=acc[:], func=GATE_FUNC[gate], bias=bias_sb[:, col : col + 1], scale=1.0)
+                r[gate] = gate_sb
+                if gate == "i":
+                    tanh_cand = gate_pool.tile([P, n], F32)
+                    nc.scalar.activation(out=tanh_cand[:], in_=r["cand"][:], func=ACT.Tanh)
+                    r["tc"] = tanh_cand
+                    if r["prod"] == "G":
+                        product_ci(r, nc.gpsimd)
+                if gate == "o" and r["prod"] == "G":
+                    product_h(r, nc.gpsimd)
+
+        def product_ci(r, engine):
+            cand_i = gate_pool.tile([P, r["nt"] * P], F32)
+            engine.tensor_tensor(out=cand_i[:], in0=r["cand"][:], in1=r["i"][:], op=ALU.mult)
+            r["ci"] = cand_i
+
+        def product_h(r, engine):
+            h_turned = gate_pool.tile([P, r["nt"] * P], F32)
+            engine.tensor_tensor(out=h_turned[:], in0=r["o"][:], in1=r["tc"][:], op=ALU.mult)
+            r["h"] = h_turned
+
+        def turn_back(r, src):
+            back = psum.tile([P, r["nt"], P], F32, tag="bank")
+            for t in range(r["nt"]):
+                nc.tensor.transpose(back[:, t, :], src[:, t * P : (t + 1) * P], ident[:])
+            return back
+
+        def where(r):
+            return slice(r["t0"], r["t0"] + r["nt"]), slice(r["half"] * P, (r["half"] + 1) * P)
+
+        def finish_h(r, engine):
+            ts, cols = where(r)
+            h_back = turn_back(r, r["h"])
+            copy_out(outs[r["c"]][0][:, ts, cols], h_back[:], engine)
+
+        def finish_f(r):
+            ts, cols = where(r)
+            f_back = turn_back(r, r["f"])
+            f_cell = out_pool.tile([P, r["nt"], P], F32)
+            nc.vector.tensor_tensor(out=f_cell[:], in0=f_back[:], in1=cell_rows[r["c"]][:, ts, cols], op=ALU.mult)
+            r["f_cell"] = f_cell
+
+        def finish_c(r):
+            ts, cols = where(r)
+            ci_back = turn_back(r, r["ci"])
+            nc.vector.tensor_tensor(out=outs[r["c"]][1][:, ts, cols], in0=ci_back[:], in1=r["f_cell"][:], op=ALU.add)
+
+        def store(r, which):
+            c = r["c"]
+            ts, cols = where(r)
+            rows = slice(c * CHUNK, (c + 1) * CHUNK)
+            dram = (out_0, out_1)[which]
+            nc.sync.dma_start(out=dram[rows, :].rearrange("(p t) h -> p t h", t=ROW_TILES)[:, ts, :], in_=outs[c][which][:, ts, :])
+
+        gw = turn_w(GATES[0], 0, "S")
+        quantise_w(GATES[0], 0, gw)
+        gz = [turn_z(number, "VS") for number in range(PASSES)]
+        for grouped in gz:
+            quantise_z(grouped)
+        for gate in GATES[1:]:
+            gw = turn_w(gate, 0, "S")
+            quantise_w(gate, 0, gw)
+
+        rounds = []
+        for c in range(N_CHUNKS):
+            pieces = TAIL_PIECES if c == N_CHUNKS - 1 else ((0, ROW_TILES),)
+            for t0, nt in pieces:
+                for half in range(HALVES):
+                    rounds.append({"c": c, "half": half, "t0": t0, "nt": nt, "order": GATES, "prod": "G"})
+        for r in rounds[len(rounds) - V_TAIL:]:
+            r["prod"] = "V"
+            r["order"] = LAST_GATES
+        outs = {}
         before = None
-        for s in range(N_ROUNDS + 1):
-            if s < N_ROUNDS:
-                c, half = divmod(s, HALVES)
-                if half == 0:
+        for s, r in enumerate(rounds + [None]):
+            if r is not None:
+                if r["c"] not in outs:
                     h_sb = out_pool.tile([P, ROW_TILES, HID], F32)
                     c_sb = out_pool.tile([P, ROW_TILES, HID], F32)
-                f_gate, cand_i, h_turned = compute_gates(c, half)
+                    outs[r["c"]] = (h_sb, c_sb)
+                compute_gates(r)
+            if s == 0:
+                for gate in GATES:
+                    gw = turn_w(gate, 1, W1_ENG[GATES.index(gate)])
+                    quantise_w(gate, 1, gw)
+            if before is not None and before["prod"] == "G":
+                finish_h(before, "V" if before["half"] == 0 else "S")
+                finish_f(before)
+            if before is not None and before["prod"] == "V":
+                finish_f(before)
+            fresh = [turn_z(number, Z_ENG.get(number, "VV")) for number in range(len(z_codes), min(s + AHEAD, N_PIECES - 1) + 1)]
             if before is not None:
-                f_cell = finish_h_and_f(before["c"], before["half"], before["f_gate"], before["h_turned"], before["h_sb"])
-            fresh = [
-                turn_z_pass(number, ())
-                for number in range(len(z_codes), min(s + AHEAD, N_Z_PASSES - 1) + 1)
-            ]
-            if before is not None:
-                finish_c(before["c"], before["half"], before["cand_i"], f_cell, before["c_sb"])
-            for grouped in fresh:
-                quantise_z_pass(grouped)
+                finish_c(before)
+                if before["half"] == HALVES - 1:
+                    store(before, 1)
+            if before is not None and before["prod"] == "V":
+                finish_h(before, "S")
             if before is not None and before["half"] == HALVES - 1:
-                store(before["c"], before["h_sb"], before["c_sb"])
-            before = {
-                "c": c, "half": half, "f_gate": f_gate, "cand_i": cand_i, "h_turned": h_turned,
-                "h_sb": h_sb, "c_sb": c_sb,
-            }
+                store(before, 0)
+            for grouped in fresh:
+                quantise_z(grouped)
+            if r is not None and r["prod"] == "V":
+                product_ci(r, nc.vector)
+                product_h(r, nc.vector)
+            before = r

@@ -31,6 +31,7 @@ FLOPS = 2 * BATCH * K * 4 * HID
 AHEAD = 3
 TAIL_PIECES = ((0, 4),)
 V_TAIL = 0
+N_WARM = 0
 W1_ENG = "VSVS"
 Z_ENG = {2: "SS", 3: "SV"}
 N_ROUNDS = N_CHUNKS * HALVES
@@ -99,12 +100,21 @@ def tile_quest_pa_t_kernel(tc, X, hidden1, cell1, Wf1, bf1, Wi1, bi1, Wc1, bc1, 
         nc.vector.memset(warm_in[:], 0.0)
         nc.scalar.activation(out=warm_out[:], in_=warm_in[:], func=ACT.Sigmoid)
 
-        bias_rows_f32 = const.tile([P, P], F32)
-        nc.vector.tensor_copy(out=bias_rows_f32[:], in_=bias_rows[:])
-        bias_ps = psum.tile([P, P], F32, tag="bank")
-        nc.tensor.transpose(bias_ps[:], bias_rows_f32[:], ident[:])
+        ident_bf = const.tile([P, P], BF16)
+        make_identity(nc, ident_bf[:])
         bias_sb = const.tile([P, HALVES * len(GATES)], F32)
-        nc.vector.tensor_copy(out=bias_sb[:], in_=bias_ps[:, 0 : HALVES * len(GATES)])
+
+        def turn_biases():
+            bias_ps = psum.tile([P, P], BF16, tag="bank")
+            nc.tensor.transpose(bias_ps[:], bias_rows[:], ident_bf[:])
+            nc.scalar.copy(out=bias_sb[:], in_=bias_ps[:, 0 : HALVES * len(GATES)])
+
+        if N_WARM:
+            warm_sb = const.tile([P, CHUNK], BF16)
+            nc.vector.memset(warm_sb[:], 1.0)
+            warm_ps = psum.tile([P, CHUNK], F32, tag="bank")
+            for w in range(N_WARM):
+                nc.tensor.matmul(out=warm_ps[:], lhsT=warm_sb[:, 0:P], rhs=warm_sb[:], start=True, stop=True)
 
         def copy_out(dst, src, engine):
             if engine == "S":
@@ -226,6 +236,7 @@ def tile_quest_pa_t_kernel(tc, X, hidden1, cell1, Wf1, bf1, Wi1, bi1, Wc1, bc1, 
         gw = turn_w(GATES[0], 0, "S")
         quantise_w(GATES[0], 0, gw)
         gz = [turn_z(number, "VS") for number in range(PASSES)]
+        turn_biases()
         for grouped in gz:
             quantise_z(grouped)
         for gate in GATES[1:]:

@@ -31,7 +31,8 @@ FLOPS = 2 * BATCH * K * 4 * HID
 AHEAD = 3
 TAIL_PIECES = ((0, 4),)
 V_TAIL = 0
-N_WARM = 0
+N_WARM = 8
+N_WARM2 = 4
 W1_ENG = "VSVS"
 Z_ENG = {2: "SS", 3: "SV"}
 N_ROUNDS = N_CHUNKS * HALVES
@@ -109,12 +110,16 @@ def tile_quest_pa_t_kernel(tc, X, hidden1, cell1, Wf1, bf1, Wi1, bi1, Wc1, bc1, 
             nc.tensor.transpose(bias_ps[:], bias_rows[:], ident_bf[:])
             nc.scalar.copy(out=bias_sb[:], in_=bias_ps[:, 0 : HALVES * len(GATES)])
 
-        if N_WARM:
-            warm_sb = const.tile([P, CHUNK], BF16)
-            nc.vector.memset(warm_sb[:], 1.0)
+        warm_sb = const.tile([P, CHUNK], BF16)
+        nc.vector.memset(warm_sb[:], 1.0)
+
+        def keep_warm(n):
             warm_ps = psum.tile([P, CHUNK], F32, tag="bank")
-            for w in range(N_WARM):
+            for w in range(n):
                 nc.tensor.matmul(out=warm_ps[:], lhsT=warm_sb[:, 0:P], rhs=warm_sb[:], start=True, stop=True)
+
+        if N_WARM:
+            keep_warm(N_WARM)
 
         def copy_out(dst, src, engine):
             if engine == "S":
@@ -235,6 +240,8 @@ def tile_quest_pa_t_kernel(tc, X, hidden1, cell1, Wf1, bf1, Wi1, bi1, Wc1, bc1, 
 
         gw = turn_w(GATES[0], 0, "S")
         quantise_w(GATES[0], 0, gw)
+        if N_WARM2:
+            keep_warm(N_WARM2)
         gz = [turn_z(number, "VS") for number in range(PASSES)]
         turn_biases()
         for grouped in gz:

@@ -29,8 +29,8 @@ LAST_GATES = ("cand", "i", "f", "o")
 GATE_FUNC = {"cand": ACT.Tanh, "i": ACT.Sigmoid, "o": ACT.Sigmoid, "f": ACT.Sigmoid}
 FLOPS = 2 * BATCH * K * 4 * HID
 AHEAD = 3
-TAIL_PIECES = ((0, 4),)
-V_TAIL = 0
+TAIL_PIECES = ((0, 2), (2, 2))
+V_TAIL = 2
 N_WARM = 8
 N_WARM2 = 4
 W1_ENG = "VSVS"

@@ -33,6 +33,14 @@ TAIL_PIECES = ((0, 2), (2, 2))
 V_TAIL = 2
 N_WARM = 8
 N_WARM2 = 4
+CI_ENG = "V"
+H_ENG = "G"
+H_COPY = "SS"
+Z_DEF = "VV"
+GROUP = 1
+GROUP_FROM = 2
+GROUP_TAIL = 4
+RES_BUFS = 2
 W1_ENG = "VSVS"
 Z_ENG = {2: "SS", 3: "SV"}
 N_ROUNDS = N_CHUNKS * HALVES
@@ -182,7 +190,7 @@ def tile_quest_pa_t_kernel(tc, X, hidden1, cell1, Wf1, bf1, Wi1, bi1, Wc1, bc1, 
                     nc.tensor.matmul_mx(out=acc[:], lhsT=w_codes[:, gi, half, g, :].bitcast(FP8X4), lhsT_scale=w_scales[:, gi, half, g, :],
                                         rhs=z_codes[PASSES * c + g][:, batch].bitcast(FP8X4), rhs_scale=z_scales[PASSES * c + g][:, batch],
                                         start=(g == 0), stop=(g == PASSES - 1))
-                gate_sb = gate_pool.tile([P, n], F32, tag="gate_" + gate)
+                gate_sb = gate_pool.tile([P, n], F32, tag="gate_" + gate, bufs=RES_BUFS if gate == "f" else 2)
                 col = HALVES * gi + half
                 nc.scalar.activation(out=gate_sb[:], in_=acc[:], func=GATE_FUNC[gate], bias=bias_sb[:, col : col + 1], scale=1.0)
                 r[gate] = gate_sb
@@ -191,17 +199,17 @@ def tile_quest_pa_t_kernel(tc, X, hidden1, cell1, Wf1, bf1, Wi1, bi1, Wc1, bc1, 
                     nc.scalar.activation(out=tanh_cand[:], in_=r["cand"][:], func=ACT.Tanh)
                     r["tc"] = tanh_cand
                     if r["prod"] == "G":
-                        product_ci(r, nc.gpsimd)
+                        product_ci(r, nc.gpsimd if CI_ENG == "G" else nc.vector)
                 if gate == "o" and r["prod"] == "G":
-                    product_h(r, nc.gpsimd)
+                    product_h(r, nc.gpsimd if H_ENG == "G" else nc.vector)
 
         def product_ci(r, engine):
-            cand_i = gate_pool.tile([P, r["nt"] * P], F32)
+            cand_i = gate_pool.tile([P, r["nt"] * P], F32, bufs=RES_BUFS)
             engine.tensor_tensor(out=cand_i[:], in0=r["cand"][:], in1=r["i"][:], op=ALU.mult)
             r["ci"] = cand_i
 
         def product_h(r, engine):
-            h_turned = gate_pool.tile([P, r["nt"] * P], F32)
+            h_turned = gate_pool.tile([P, r["nt"] * P], F32, bufs=RES_BUFS)
             engine.tensor_tensor(out=h_turned[:], in0=r["o"][:], in1=r["tc"][:], op=ALU.mult)
             r["h"] = h_turned
 
@@ -260,35 +268,51 @@ def tile_quest_pa_t_kernel(tc, X, hidden1, cell1, Wf1, bf1, Wi1, bi1, Wc1, bc1, 
             r["prod"] = "V"
             r["order"] = LAST_GATES
         outs = {}
-        before = None
-        for s, r in enumerate(rounds + [None]):
-            if r is not None:
+        steps = []
+        s = 0
+        done = 0
+        while done < len(rounds):
+            width = GROUP if GROUP_FROM <= s and s + GROUP <= len(rounds) - GROUP_TAIL else 1
+            comp = list(range(s, min(s + width, len(rounds))))
+            fin = list(range(done, s))
+            steps.append((comp, fin))
+            done = s
+            s += len(comp)
+        for comp, fin in steps:
+            for s in comp:
+                r = rounds[s]
                 if r["c"] not in outs:
                     h_sb = out_pool.tile([P, ROW_TILES, HID], F32)
                     c_sb = out_pool.tile([P, ROW_TILES, HID], F32)
                     outs[r["c"]] = (h_sb, c_sb)
                 compute_gates(r)
-            if s == 0:
+            if comp and comp[0] == 0:
                 for gate in GATES:
                     gw = turn_w(gate, 1, W1_ENG[GATES.index(gate)])
                     quantise_w(gate, 1, gw)
-            if before is not None and before["prod"] == "G":
-                finish_h(before, "V" if before["half"] == 0 else "S")
-                finish_f(before)
-            if before is not None and before["prod"] == "V":
-                finish_f(before)
-            fresh = [turn_z(number, Z_ENG.get(number, "VV")) for number in range(len(z_codes), min(s + AHEAD, N_PIECES - 1) + 1)]
-            if before is not None:
-                finish_c(before)
-                if before["half"] == HALVES - 1:
-                    store(before, 1)
-            if before is not None and before["prod"] == "V":
-                finish_h(before, "S")
-            if before is not None and before["half"] == HALVES - 1:
-                store(before, 0)
-            for grouped in fresh:
-                quantise_z(grouped)
-            if r is not None and r["prod"] == "V":
-                product_ci(r, nc.vector)
-                product_h(r, nc.vector)
-            before = r
+            top = (comp[-1] if comp else len(rounds)) + AHEAD
+            numbers = list(range(len(z_codes), min(top, N_PIECES - 1) + 1))
+            slots = max(len(fin), 1)
+            for k in range(slots):
+                before = rounds[fin[k]] if fin else None
+                mine = numbers[k * len(numbers) // slots : (k + 1) * len(numbers) // slots]
+                if before is not None and before["prod"] == "G":
+                    finish_h(before, H_COPY[before["half"]])
+                    finish_f(before)
+                if before is not None and before["prod"] == "V":
+                    finish_f(before)
+                fresh = [turn_z(number, Z_ENG.get(number, Z_DEF)) for number in mine]
+                if before is not None:
+                    finish_c(before)
+                    if before["half"] == HALVES - 1:
+                        store(before, 1)
+                if before is not None and before["prod"] == "V":
+                    finish_h(before, "S")
+                if before is not None and before["half"] == HALVES - 1:
+                    store(before, 0)
+                for grouped in fresh:
+                    quantise_z(grouped)
+            for s in comp:
+                if rounds[s]["prod"] == "V":
+                    product_ci(rounds[s], nc.vector)
+                    product_h(rounds[s], nc.vector)

@@ -28,7 +28,7 @@ GATES = ("cand", "i", "o", "f")
 LAST_GATES = ("cand", "i", "f", "o")
 GATE_FUNC = {"cand": ACT.Tanh, "i": ACT.Sigmoid, "o": ACT.Sigmoid, "f": ACT.Sigmoid}
 FLOPS = 2 * BATCH * K * 4 * HID
-AHEAD = 3
+AHEAD = 4
 TAIL_PIECES = ((0, 2), (2, 2))
 V_TAIL = 2
 N_WARM = 8
@@ -37,10 +37,13 @@ CI_ENG = "V"
 H_ENG = "G"
 H_COPY = "SS"
 Z_DEF = "VV"
-GROUP = 1
+GROUP = 2
+DEFER = 1
+H_LAST = 1
+GATE_BUFS = 2
 GROUP_FROM = 2
 GROUP_TAIL = 4
-RES_BUFS = 2
+RES_BUFS = 4
 W1_ENG = "VSVS"
 Z_ENG = {2: "SS", 3: "SV"}
 N_ROUNDS = N_CHUNKS * HALVES
@@ -190,18 +193,21 @@ def tile_quest_pa_t_kernel(tc, X, hidden1, cell1, Wf1, bf1, Wi1, bi1, Wc1, bc1, 
                     nc.tensor.matmul_mx(out=acc[:], lhsT=w_codes[:, gi, half, g, :].bitcast(FP8X4), lhsT_scale=w_scales[:, gi, half, g, :],
                                         rhs=z_codes[PASSES * c + g][:, batch].bitcast(FP8X4), rhs_scale=z_scales[PASSES * c + g][:, batch],
                                         start=(g == 0), stop=(g == PASSES - 1))
-                gate_sb = gate_pool.tile([P, n], F32, tag="gate_" + gate, bufs=RES_BUFS if gate == "f" else 2)
+                gate_sb = gate_pool.tile([P, n], F32, tag="gate_" + gate, bufs=RES_BUFS if gate == "f" else GATE_BUFS)
                 col = HALVES * gi + half
                 nc.scalar.activation(out=gate_sb[:], in_=acc[:], func=GATE_FUNC[gate], bias=bias_sb[:, col : col + 1], scale=1.0)
                 r[gate] = gate_sb
-                if gate == "i":
-                    tanh_cand = gate_pool.tile([P, n], F32)
-                    nc.scalar.activation(out=tanh_cand[:], in_=r["cand"][:], func=ACT.Tanh)
-                    r["tc"] = tanh_cand
+                if gate == "i" and not r["defer"]:
+                    second_tanh(r)
                     if r["prod"] == "G":
                         product_ci(r, nc.gpsimd if CI_ENG == "G" else nc.vector)
-                if gate == "o" and r["prod"] == "G":
+                if gate == "o" and r["prod"] == "G" and not r["defer"]:
                     product_h(r, nc.gpsimd if H_ENG == "G" else nc.vector)
+
+        def second_tanh(r):
+            tanh_cand = gate_pool.tile([P, r["nt"] * P], F32)
+            nc.scalar.activation(out=tanh_cand[:], in_=r["cand"][:], func=ACT.Tanh)
+            r["tc"] = tanh_cand
 
         def product_ci(r, engine):
             cand_i = gate_pool.tile([P, r["nt"] * P], F32, bufs=RES_BUFS)
@@ -263,10 +269,18 @@ def tile_quest_pa_t_kernel(tc, X, hidden1, cell1, Wf1, bf1, Wi1, bi1, Wc1, bc1, 
             pieces = TAIL_PIECES if c == N_CHUNKS - 1 else ((0, ROW_TILES),)
             for t0, nt in pieces:
                 for half in range(HALVES):
-                    rounds.append({"c": c, "half": half, "t0": t0, "nt": nt, "order": GATES, "prod": "G"})
+                    rounds.append({"c": c, "half": half, "t0": t0, "nt": nt, "order": GATES, "prod": "G", "defer": False})
         for r in rounds[len(rounds) - V_TAIL:]:
             r["prod"] = "V"
             r["order"] = LAST_GATES
+        def deferred(comp):
+            for s in comp:
+                r = rounds[s]
+                if r["defer"]:
+                    second_tanh(r)
+                    product_ci(r, nc.gpsimd if CI_ENG == "G" else nc.vector)
+                    product_h(r, nc.gpsimd if H_ENG == "G" else nc.vector)
+
         outs = {}
         steps = []
         s = 0
@@ -285,33 +299,37 @@ def tile_quest_pa_t_kernel(tc, X, hidden1, cell1, Wf1, bf1, Wi1, bi1, Wc1, bc1, 
                     h_sb = out_pool.tile([P, ROW_TILES, HID], F32)
                     c_sb = out_pool.tile([P, ROW_TILES, HID], F32)
                     outs[r["c"]] = (h_sb, c_sb)
+                r["defer"] = DEFER and len(comp) > 1
                 compute_gates(r)
+            if DEFER == 1:
+                deferred(comp)
             if comp and comp[0] == 0:
                 for gate in GATES:
                     gw = turn_w(gate, 1, W1_ENG[GATES.index(gate)])
                     quantise_w(gate, 1, gw)
-            top = (comp[-1] if comp else len(rounds)) + AHEAD
+            top = (comp[-1] if comp else len(rounds)) + (AHEAD if comp and comp[0] >= 1 else 3)
             numbers = list(range(len(z_codes), min(top, N_PIECES - 1) + 1))
             slots = max(len(fin), 1)
             for k in range(slots):
                 before = rounds[fin[k]] if fin else None
                 mine = numbers[k * len(numbers) // slots : (k + 1) * len(numbers) // slots]
-                if before is not None and before["prod"] == "G":
+                if before is not None and before["prod"] == "G" and not H_LAST:
                     finish_h(before, H_COPY[before["half"]])
-                    finish_f(before)
-                if before is not None and before["prod"] == "V":
+                if before is not None:
                     finish_f(before)
                 fresh = [turn_z(number, Z_ENG.get(number, Z_DEF)) for number in mine]
                 if before is not None:
                     finish_c(before)
                     if before["half"] == HALVES - 1:
                         store(before, 1)
-                if before is not None and before["prod"] == "V":
+                if before is not None and (before["prod"] == "V" or H_LAST):
                     finish_h(before, "S")
                 if before is not None and before["half"] == HALVES - 1:
                     store(before, 0)
                 for grouped in fresh:
                     quantise_z(grouped)
+            if DEFER == 2:
+                deferred(comp)
             for s in comp:
                 if rounds[s]["prod"] == "V":
                     product_ci(rounds[s], nc.vector)

@@ -32,17 +32,19 @@ AHEAD = 4
 TAIL_PIECES = ((0, 2), (2, 2))
 V_TAIL = 2
 N_WARM = 8
-N_WARM2 = 4
+N_WARM2 = 0
 CI_ENG = "V"
 H_ENG = "G"
 H_COPY = "SS"
 Z_DEF = "VV"
 GROUP = 2
+G_PARTS = 1
+V_HEAD = 0
 DEFER = 1
 H_LAST = 1
 GATE_BUFS = 2
 GROUP_FROM = 2
-GROUP_TAIL = 4
+GROUP_TAIL = 2
 RES_BUFS = 4
 W1_ENG = "VSVS"
 Z_ENG = {2: "SS", 3: "SV"}
@@ -216,7 +218,11 @@ def tile_quest_pa_t_kernel(tc, X, hidden1, cell1, Wf1, bf1, Wi1, bi1, Wc1, bc1, 
 
         def product_h(r, engine):
             h_turned = gate_pool.tile([P, r["nt"] * P], F32, bufs=RES_BUFS)
-            engine.tensor_tensor(out=h_turned[:], in0=r["o"][:], in1=r["tc"][:], op=ALU.mult)
+            n = r["nt"] * P
+            parts = G_PARTS if engine == nc.gpsimd else 1
+            for q in range(parts):
+                cols = slice(q * n // parts, (q + 1) * n // parts)
+                engine.tensor_tensor(out=h_turned[:, cols], in0=r["o"][:, cols], in1=r["tc"][:, cols], op=ALU.mult)
             r["h"] = h_turned
 
         def turn_back(r, src):
@@ -270,6 +276,8 @@ def tile_quest_pa_t_kernel(tc, X, hidden1, cell1, Wf1, bf1, Wi1, bi1, Wc1, bc1, 
             for t0, nt in pieces:
                 for half in range(HALVES):
                     rounds.append({"c": c, "half": half, "t0": t0, "nt": nt, "order": GATES, "prod": "G", "defer": False})
+        for r in rounds[0:V_HEAD]:
+            r["prod"] = "V"
         for r in rounds[len(rounds) - V_TAIL:]:
             r["prod"] = "V"
             r["order"] = LAST_GATES

@@ -39,6 +39,7 @@ H_COPY = "SS"
 Z_DEF = "VV"
 GROUP = 2
 G_PARTS = 1
+TAIL_H = "SSSS"
 V_HEAD = 0
 DEFER = 1
 H_LAST = 1
@@ -77,10 +78,11 @@ def tile_quest_pa_t_kernel(tc, X, hidden1, cell1, Wf1, bf1, Wi1, bi1, Wc1, bc1, 
 
         def load_z(c):
             rows = slice(c * CHUNK, (c + 1) * CHUNK)
-            z_sb = in_pool.tile([P, ROW_TILES, K], BF16)
-            nc.sync.dma_start(out=z_sb[:, :, 0:N_X], in_=X[rows, :].rearrange("(p t) k -> p t k", t=ROW_TILES))
-            nc.sync.dma_start(out=z_sb[:, :, N_X:K], in_=hidden1[rows, :].rearrange("(p t) k -> p t k", t=ROW_TILES))
-            z_rows.append(z_sb)
+            x_sb = in_pool.tile([P, ROW_TILES, N_X], BF16)
+            nc.sync.dma_start(out=x_sb[:], in_=X[rows, :].rearrange("(p t) k -> p t k", t=ROW_TILES))
+            hid_sb = in_pool.tile([P, ROW_TILES, K - N_X], BF16)
+            nc.sync.dma_start(out=hid_sb[:], in_=hidden1[rows, :].rearrange("(p t) k -> p t k", t=ROW_TILES))
+            z_rows.append((x_sb, hid_sb))
 
         def load_cell(c):
             rows = slice(c * CHUNK, (c + 1) * CHUNK)
@@ -151,8 +153,10 @@ def tile_quest_pa_t_kernel(tc, X, hidden1, cell1, Wf1, bf1, Wi1, bi1, Wc1, bc1, 
                 turned = psum.tile([P, 2, 2 * P], F32, tag="bank")
                 for u in range(2):
                     first = PASS_WORDS * g + P * u
+                    source = 0 if first < N_X // 2 else 1
+                    first -= source * (N_X // 2)
                     for r in range(2):
-                        src_words = z_rows[c][:, 2 * pair + r, :].bitcast(F32)
+                        src_words = z_rows[c][source][:, 2 * pair + r, :].bitcast(F32)
                         nc.tensor.transpose(turned[:, u, r * P : (r + 1) * P], src_words[:, first : first + P], ident[:])
                 copy_out(words[:, 2 * pair * P : 2 * (pair + 1) * P, :], turned[:].rearrange("p u j -> p j u"), engines[pair])
             return grouped
@@ -331,7 +335,7 @@ def tile_quest_pa_t_kernel(tc, X, hidden1, cell1, Wf1, bf1, Wi1, bi1, Wc1, bc1, 
                     if before["half"] == HALVES - 1:
                         store(before, 1)
                 if before is not None and (before["prod"] == "V" or H_LAST):
-                    finish_h(before, "S")
+                    finish_h(before, TAIL_H[fin[k] - (len(rounds) - len(TAIL_H))] if fin[k] >= len(rounds) - len(TAIL_H) else "S")
                 if before is not None and before["half"] == HALVES - 1:
                     store(before, 0)
                 for grouped in fresh:

from contextlib import ExitStack

import concourse.mybir as mybir
from concourse.masks import make_identity

F32 = mybir.dt.float32
BF16 = mybir.dt.bfloat16
U32 = mybir.dt.uint32
U8 = mybir.dt.uint8
FP8X4 = mybir.dt.float8_e4m3fn_x4
ACT = mybir.ActivationFunctionType
ALU = mybir.AluOpType

P = 128
PACK = 4
K = 1024
N_X = 768
K_PASS = P * PACK
PASSES = K // K_PASS
PASS_WORDS = K_PASS // 2
BATCH = 4096
CHUNK = 512
ROW_TILES = CHUNK // P
N_CHUNKS = BATCH // CHUNK
HID = 256
HALVES = HID // P
GATES = ("cand", "i", "o", "f")
LAST_GATES = ("cand", "i", "f", "o")
GATE_FUNC = {"cand": ACT.Tanh, "i": ACT.Sigmoid, "o": ACT.Sigmoid, "f": ACT.Sigmoid}
FLOPS = 2 * BATCH * K * 4 * HID
AHEAD = 4
TAIL_PIECES = ((0, 2), (2, 2))
V_TAIL = 2
N_WARM = 8
N_WARM2 = 0
CI_ENG = "V"
H_ENG = "G"
H_COPY = "SS"
Z_DEF = "VV"
GROUP = 2
G_PARTS = 1
TAIL_H = "SSSS"
V_HEAD = 0
DEFER = 1
H_LAST = 1
GATE_BUFS = 2
GROUP_FROM = 2
GROUP_TAIL = 2
RES_BUFS = 4
W1_ENG = "VSVS"
Z_ENG = {2: "SS", 3: "SV"}
N_ROUNDS = N_CHUNKS * HALVES
N_PIECES = N_CHUNKS * PASSES


def tile_quest_pa_t_kernel(tc, X, hidden1, cell1, Wf1, bf1, Wi1, bi1, Wc1, bc1, Wo1, bo1, out_0, out_1):
    nc = tc.nc
    weights = {"f": Wf1, "i": Wi1, "cand": Wc1, "o": Wo1}
    biases = {"f": bf1, "i": bi1, "cand": bc1, "o": bo1}
    with ExitStack() as stack:
        stack.enter_context(tc.manual_schedule())
        const = stack.enter_context(tc.tile_pool(name="const", bufs=1))
        w_pool = stack.enter_context(tc.tile_pool(name="w_raw", bufs=len(GATES) * HALVES))
        in_pool = stack.enter_context(tc.tile_pool(name="inputs", bufs=N_CHUNKS))
        grouped_pool = stack.enter_context(tc.tile_pool(name="grouped", bufs=3))
        codes_pool = stack.enter_context(tc.tile_pool(name="codes", bufs=PASSES + AHEAD))
        gate_pool = stack.enter_context(tc.tile_pool(name="gates", bufs=2))
        out_pool = stack.enter_context(tc.tile_pool(name="outs", bufs=3))
        psum = stack.enter_context(tc.psum_pool(name="psum", bufs=8))

        bias_rows = const.tile([P, P], BF16)
        nc.vector.memset(bias_rows[:], 0.0)
        for gi, gate in enumerate(GATES):
            nc.scalar.dma_start(out=bias_rows[HALVES * gi : HALVES * (gi + 1), :], in_=biases[gate].rearrange("(e p) -> e p", p=P))

        z_rows = []
        cell_rows = []

        def load_z(c):
            rows = slice(c * CHUNK, (c + 1) * CHUNK)
            x_sb = in_pool.tile([P, ROW_TILES, N_X], BF16)
            nc.sync.dma_start(out=x_sb[:], in_=X[rows, :].rearrange("(p t) k -> p t k", t=ROW_TILES))
            hid_sb = in_pool.tile([P, ROW_TILES, K - N_X], BF16)
            nc.sync.dma_start(out=hid_sb[:], in_=hidden1[rows, :].rearrange("(p t) k -> p t k", t=ROW_TILES))
            z_rows.append((x_sb, hid_sb))

        def load_cell(c):
            rows = slice(c * CHUNK, (c + 1) * CHUNK)
            cell_sb = in_pool.tile([P, ROW_TILES, HID], BF16)
            nc.sync.dma_start(out=cell_sb[:], in_=cell1[rows, :].rearrange("(p t) h -> p t h", t=ROW_TILES))
            cell_rows.append(cell_sb)


        w_rows = {}

        def load_w(gate, half):
            w_sb = w_pool.tile([P, K], BF16)
            nc.sync.dma_start(out=w_sb[:], in_=weights[gate][half * P : (half + 1) * P, :])
            w_rows[gate, half] = w_sb

        load_w(GATES[0], 0)
        load_z(0)
        for gate in GATES[1:]:
            load_w(gate, 0)
        for gate in GATES:
            load_w(gate, 1)
        for c in range(1, N_CHUNKS):
            load_z(c)
            load_cell(c - 1)
        load_cell(N_CHUNKS - 1)

        ident = const.tile([P, P], F32)
        make_identity(nc, ident[:])
        warm_in = const.tile([P, 1], F32)
        warm_out = const.tile([P, 1], F32)
        nc.vector.memset(warm_in[:], 0.0)
        nc.scalar.activation(out=warm_out[:], in_=warm_in[:], func=ACT.Sigmoid)

        ident_bf = const.tile([P, P], BF16)
        make_identity(nc, ident_bf[:])
        bias_sb = const.tile([P, HALVES * len(GATES)], F32)

        def turn_biases():
            bias_ps = psum.tile([P, P], BF16, tag="bank")
            nc.tensor.transpose(bias_ps[:], bias_rows[:], ident_bf[:])
            nc.scalar.copy(out=bias_sb[:], in_=bias_ps[:, 0 : HALVES * len(GATES)])

        warm_sb = const.tile([P, CHUNK], BF16)
        nc.vector.memset(warm_sb[:], 1.0)

        def keep_warm(n):
            warm_ps = psum.tile([P, CHUNK], F32, tag="bank")
            for w in range(n):
                nc.tensor.matmul(out=warm_ps[:], lhsT=warm_sb[:, 0:P], rhs=warm_sb[:], start=True, stop=True)

        if N_WARM:
            keep_warm(N_WARM)

        def copy_out(dst, src, engine):
            if engine == "S":
                nc.scalar.copy(out=dst, in_=src)
            else:
                nc.vector.tensor_copy(out=dst, in_=src)

        z_codes = []
        z_scales = []

        def turn_z(number, engines):
            c, g = divmod(number, PASSES)
            grouped = grouped_pool.tile([P, CHUNK * PACK], BF16, align_bytes=64)
            words = grouped[:].bitcast(F32).rearrange("p (j u) -> p j u", u=2)
            for pair in range(ROW_TILES // 2):
                turned = psum.tile([P, 2, 2 * P], F32, tag="bank")
                for u in range(2):
                    first = PASS_WORDS * g + P * u
                    source = 0 if first < N_X // 2 else 1
                    first -= source * (N_X // 2)
                    for r in range(2):
                        src_words = z_rows[c][source][:, 2 * pair + r, :].bitcast(F32)
                        nc.tensor.transpose(turned[:, u, r * P : (r + 1) * P], src_words[:, first : first + P], ident[:])
                copy_out(words[:, 2 * pair * P : 2 * (pair + 1) * P, :], turned[:].rearrange("p u j -> p j u"), engines[pair])
            return grouped

        def quantise_z(grouped):
            codes = codes_pool.tile([P, CHUNK], U32, align_bytes=64)
            scales = codes_pool.tile([P, CHUNK], U8, align_bytes=64)
            nc.vector.quantize_mx(out=codes[:].bitcast(FP8X4), scales=scales[:], in_=grouped[:])
            z_codes.append(codes)
            z_scales.append(scales)

        w_codes = const.tile([P, len(GATES), HALVES, PASSES, P], U32, align_bytes=64)
        w_scales = const.tile([P, len(GATES), HALVES, PASSES, P], U8, align_bytes=64)

        def turn_w(gate, half, engine):
            grouped_w = grouped_pool.tile([P, PASSES * P * PACK], BF16, align_bytes=64, bufs=4)
            turned = psum.tile([P, PASSES, 2, P], F32, tag="bank")
            src_words = w_rows[gate, half][:].bitcast(F32)
            for g in range(PASSES):
                for u in range(2):
                    first = PASS_WORDS * g + P * u
                    nc.tensor.transpose(turned[:, g, u, :], src_words[:, first : first + P], ident[:])
            copy_out(grouped_w[:].bitcast(F32).rearrange("p (g j u) -> p g j u", g=PASSES, u=2), turned[:].rearrange("p g u j -> p g j u"), engine)
            return grouped_w

        def quantise_w(gate, half, grouped_w):
            gi = GATES.index(gate)
            nc.vector.quantize_mx(
                out=w_codes[:, gi, half, :, :].rearrange("p g h -> p (g h)").bitcast(FP8X4),
                scales=w_scales[:, gi, half, :, :].rearrange("p g h -> p (g h)"), in_=grouped_w[:])

        def compute_gates(r):
            c, half, t0, nt = r["c"], r["half"], r["t0"], r["nt"]
            n = nt * P
            batch = slice(t0 * P, t0 * P + n)
            for gate in r["order"]:
                gi = GATES.index(gate)
                acc = psum.tile([P, n], F32, tag="bank")
                for g in range(PASSES):
                    nc.tensor.matmul_mx(out=acc[:], lhsT=w_codes[:, gi, half, g, :].bitcast(FP8X4), lhsT_scale=w_scales[:, gi, half, g, :],
                                        rhs=z_codes[PASSES * c + g][:, batch].bitcast(FP8X4), rhs_scale=z_scales[PASSES * c + g][:, batch],
                                        start=(g == 0), stop=(g == PASSES - 1))
                gate_sb = gate_pool.tile([P, n], F32, tag="gate_" + gate, bufs=RES_BUFS if gate == "f" else GATE_BUFS)
                col = HALVES * gi + half
                nc.scalar.activation(out=gate_sb[:], in_=acc[:], func=GATE_FUNC[gate], bias=bias_sb[:, col : col + 1], scale=1.0)
                r[gate] = gate_sb
                if gate == "i" and not r["defer"]:
                    second_tanh(r)
                    if r["prod"] == "G":
                        product_ci(r, nc.gpsimd if CI_ENG == "G" else nc.vector)
                if gate == "o" and r["prod"] == "G" and not r["defer"]:
                    product_h(r, nc.gpsimd if H_ENG == "G" else nc.vector)

        def second_tanh(r):
            tanh_cand = gate_pool.tile([P, r["nt"] * P], F32)
            nc.scalar.activation(out=tanh_cand[:], in_=r["cand"][:], func=ACT.Tanh)
            r["tc"] = tanh_cand

        def product_ci(r, engine):
            cand_i = gate_pool.tile([P, r["nt"] * P], F32, bufs=RES_BUFS)
            engine.tensor_tensor(out=cand_i[:], in0=r["cand"][:], in1=r["i"][:], op=ALU.mult)
            r["ci"] = cand_i

        def product_h(r, engine):
            h_turned = gate_pool.tile([P, r["nt"] * P], F32, bufs=RES_BUFS)
            n = r["nt"] * P
            parts = G_PARTS if engine == nc.gpsimd else 1
            for q in range(parts):
                cols = slice(q * n // parts, (q + 1) * n // parts)
                engine.tensor_tensor(out=h_turned[:, cols], in0=r["o"][:, cols], in1=r["tc"][:, cols], op=ALU.mult)
            r["h"] = h_turned

        def turn_back(r, src):
            back = psum.tile([P, r["nt"], P], F32, tag="bank")
            for t in range(r["nt"]):
                nc.tensor.transpose(back[:, t, :], src[:, t * P : (t + 1) * P], ident[:])
            return back

        def where(r):
            return slice(r["t0"], r["t0"] + r["nt"]), slice(r["half"] * P, (r["half"] + 1) * P)

        def finish_h(r, engine):
            ts, cols = where(r)
            h_back = turn_back(r, r["h"])
            copy_out(outs[r["c"]][0][:, ts, cols], h_back[:], engine)

        def finish_f(r):
            ts, cols = where(r)
            f_back = turn_back(r, r["f"])
            f_cell = out_pool.tile([P, r["nt"], P], F32)
            nc.vector.tensor_tensor(out=f_cell[:], in0=f_back[:], in1=cell_rows[r["c"]][:, ts, cols], op=ALU.mult)
            r["f_cell"] = f_cell

        def finish_c(r):
            ts, cols = where(r)
            ci_back = turn_back(r, r["ci"])
            nc.vector.tensor_tensor(out=outs[r["c"]][1][:, ts, cols], in0=ci_back[:], in1=r["f_cell"][:], op=ALU.add)

        def store(r, which):
            c = r["c"]
            ts, cols = where(r)
            rows = slice(c * CHUNK, (c + 1) * CHUNK)
            dram = (out_0, out_1)[which]
            nc.sync.dma_start(out=dram[rows, :].rearrange("(p t) h -> p t h", t=ROW_TILES)[:, ts, :], in_=outs[c][which][:, ts, :])

        gw = turn_w(GATES[0], 0, "S")
        quantise_w(GATES[0], 0, gw)
        if N_WARM2:
            keep_warm(N_WARM2)
        gz = [turn_z(number, "VS") for number in range(PASSES)]
        turn_biases()
        for grouped in gz:
            quantise_z(grouped)
        for gate in GATES[1:]:
            gw = turn_w(gate, 0, "S")
            quantise_w(gate, 0, gw)

        rounds = []
        for c in range(N_CHUNKS):
            pieces = TAIL_PIECES if c == N_CHUNKS - 1 else ((0, ROW_TILES),)
            for t0, nt in pieces:
                for half in range(HALVES):
                    rounds.append({"c": c, "half": half, "t0": t0, "nt": nt, "order": GATES, "prod": "G", "defer": False})
        for r in rounds[0:V_HEAD]:
            r["prod"] = "V"
        for r in rounds[len(rounds) - V_TAIL:]:
            r["prod"] = "V"
            r["order"] = LAST_GATES
        def deferred(comp):
            for s in comp:
                r = rounds[s]
                if r["defer"]:
                    second_tanh(r)
                    product_ci(r, nc.gpsimd if CI_ENG == "G" else nc.vector)
                    product_h(r, nc.gpsimd if H_ENG == "G" else nc.vector)

        outs = {}
        steps = []
        s = 0
        done = 0
        while done < len(rounds):
            width = GROUP if GROUP_FROM <= s and s + GROUP <= len(rounds) - GROUP_TAIL else 1
            comp = list(range(s, min(s + width, len(rounds))))
            fin = list(range(done, s))
            steps.append((comp, fin))
            done = s
            s += len(comp)
        for comp, fin in steps:
            for s in comp:
                r = rounds[s]
                if r["c"] not in outs:
                    h_sb = out_pool.tile([P, ROW_TILES, HID], F32)
                    c_sb = out_pool.tile([P, ROW_TILES, HID], F32)
                    outs[r["c"]] = (h_sb, c_sb)
                r["defer"] = DEFER and len(comp) > 1
                compute_gates(r)
            if DEFER == 1:
                deferred(comp)
            if comp and comp[0] == 0:
                for gate in GATES:
                    gw = turn_w(gate, 1, W1_ENG[GATES.index(gate)])
                    quantise_w(gate, 1, gw)
            top = (comp[-1] if comp else len(rounds)) + (AHEAD if comp and comp[0] >= 1 else 3)
            numbers = list(range(len(z_codes), min(top, N_PIECES - 1) + 1))
            slots = max(len(fin), 1)
            for k in range(slots):
                before = rounds[fin[k]] if fin else None
                mine = numbers[k * len(numbers) // slots : (k + 1) * len(numbers) // slots]
                if before is not None and before["prod"] == "G" and not H_LAST:
                    finish_h(before, H_COPY[before["half"]])
                if before is not None:
                    finish_f(before)
                fresh = [turn_z(number, Z_ENG.get(number, Z_DEF)) for number in mine]
                if before is not None:
                    finish_c(before)
                    if before["half"] == HALVES - 1:
                        store(before, 1)
                if before is not None and (before["prod"] == "V" or H_LAST):
                    finish_h(before, TAIL_H[fin[k] - (len(rounds) - len(TAIL_H))] if fin[k] >= len(rounds) - len(TAIL_H) else "S")
                if before is not None and before["half"] == HALVES - 1:
                    store(before, 0)
                for grouped in fresh:
                    quantise_z(grouped)
            if DEFER == 2:
                deferred(comp)
            for s in comp:
                if rounds[s]["prod"] == "V":
                    product_ci(rounds[s], nc.vector)
                    product_h(rounds[s], nc.vector)
